import numpy as np
import ml_dtypes


def mxq(x, axis, fmt="e4m3"):
    dtype, down = {"e4m3": (ml_dtypes.float8_e4m3fn, 7), "e5m2": (ml_dtypes.float8_e5m2, 14)}[fmt]
    v = np.moveaxis(np.asarray(x, np.float32).astype(ml_dtypes.bfloat16).astype(np.float64), axis, -1)
    blocks = v.reshape(v.shape[:-1] + (-1, 32))
    amax = np.abs(blocks).max(-1, keepdims=True)
    byte = np.maximum(np.where(amax > 0, np.frexp(amax)[1] - 1 + 127, 0) - down, 1)
    scale = np.exp2(byte - 127.0)
    codes = (blocks / scale).astype(np.float32).astype(dtype).astype(np.float64)
    return np.moveaxis((codes * scale).reshape(v.shape), -1, axis)


WIDE = False


def mx_kscale(k):
    if not WIDE:
        return np.ones(k)
    levels = np.array([10, -10, 5, -5, 0])
    if k % 512:
        return np.exp2(np.random.permutation(np.resize(levels, k // 32))).repeat(32)
    a = np.empty((k // 512, 16))
    for p in range(k // 512):
        a[p, :8] = np.random.permutation(np.resize(levels, 8))
        for g in range(8):
            far = levels[np.abs(levels - a[p, g]) >= 10]
            a[p, g + 8] = far[np.random.randint(len(far))]
    return np.exp2(a.ravel()).repeat(32)


BF16 = ml_dtypes.bfloat16


def bf(x):
    return np.asarray(x, np.float32).astype(BF16)


def f64(x):
    return np.asarray(x).astype(np.float64)


B, D = 2048, 1024
C = 8.0


def sigmoid(v):
    return 1.0 / (1.0 + np.exp(-v))


def softplus(v):
    return np.logaddexp(v, 0.0)


def setup_inputs():
    s = mx_kscale(D)
    xt = bf(np.random.standard_normal((B, D)) * s)
    ht_minus_1 = bf(np.random.standard_normal((B, D)) * s)
    Wa = bf(np.random.standard_normal((D, D)) / np.sqrt(D) / s[None, :])
    Wx = bf(np.random.standard_normal((D, D)) / np.sqrt(D) / s[None, :])
    ba = bf(np.random.standard_normal((1, D)) * 0.1)
    bx = bf(np.random.standard_normal((1, D)) * 0.1)
    Lambda = bf(np.random.uniform(-3.0, -1.0, (1, D)))
    return {"xt": xt, "ht_minus_1": ht_minus_1, "Wa": Wa, "Wx": Wx, "ba": ba, "bx": bx, "Lambda": Lambda}


def core(xt, ht_minus_1, Wa, Wx, ba, bx, Lambda):
    x = f64(xt)
    xq = mxq(x, 1, "e4m3")
    rt = sigmoid((xq @ mxq(f64(Wa), 1, "e4m3").T) + f64(ba))
    it = sigmoid((xq @ mxq(f64(Wx), 1, "e4m3").T) + f64(bx))
    log_at = -(C * softplus(f64(Lambda))) * rt
    at = np.exp(log_at)
    ht = at * f64(ht_minus_1) + np.sqrt(1.0 - at ** 2) * (it * x)
    return ht


def e4m3fn_bytes(y):
    return np.clip(np.asarray(y, np.float64), -448.0, 448.0).astype(np.float32).astype(ml_dtypes.float8_e4m3fn).view(np.uint8)


def reference(xt, ht_minus_1, Wa, Wx, ba, bx, Lambda):
    out = core(xt, ht_minus_1, Wa, Wx, ba, bx, Lambda)
    s = np.max(np.abs(out)) / 448.0
    return out, e4m3fn_bytes(out / s)

@@ -1,0 +1,391 @@
+from contextlib import ExitStack
+
+import concourse.mybir as mybir
+from concourse.masks import make_identity
+
+FLOPS = 2 * 2048 * 1024 * 2048
+
+F32 = mybir.dt.float32
+BF16 = mybir.dt.bfloat16
+U32 = mybir.dt.uint32
+U8 = mybir.dt.uint8
+FP8X4 = mybir.dt.float8_e4m3fn_x4
+FP8 = mybir.dt.float8_e4m3fn
+ACT = mybir.ActivationFunctionType
+ALU = mybir.AluOpType
+AX = mybir.AxisListType
+
+P = 128
+B = 2048
+D = 1024
+NJ = B // P
+NQ = 4
+NC = D // P
+VS = 2752
+SQ_ON_G = True
+RD_LAG = 3
+MX_BUFS = 4
+TP_BUFS = 4
+RUNS = ((0,), (1, 2), (3, 4), (5,), (6,), (7,))
+G_PER_WINDOW = 0
+LOOK = 2
+DEPTH = 1
+LAST_V = 1
+FX_AT = (4, 2, 2, 2)
+W_BUFS = 8
+W_ON_S = (1, 3, 5, 7)
+
+
+def tile_cell_kernel(tc, xt, ht_minus_1, Wa, Wx, ba, bx, Lambda, out_0, out_1):
+    nc = tc.nc
+    x_view = xt.rearrange("(p j) k -> p j k", j=NJ)
+    h_view = ht_minus_1.rearrange("(p j) k -> p j k", j=NJ)
+    o0_view = out_0.rearrange("(p j) c -> p j c", j=NJ)
+    o1_view = out_1.rearrange("(p j) c -> p (j c)", j=NJ)
+    w_dram = (Wa, Wx)
+
+    with ExitStack() as ctx:
+        ctx.enter_context(tc.manual_schedule(engines={mybir.EngineType.Activation}))
+        const = ctx.enter_context(tc.tile_pool(name="const", bufs=1))
+        keep = ctx.enter_context(tc.tile_pool(name="keep", bufs=1))
+        psum = ctx.enter_context(tc.psum_pool(name="psum", bufs=2))
+
+        out_sb = keep.tile([P, NJ, D], F32, name="out_sb")
+        w_codes = keep.tile([P, 2 * NC, 256], U32, name="w_codes", align_bytes=64)
+        w_scales = keep.tile([P, 2 * NC, 256], U8, name="w_scales", align_bytes=64)
+        stats = const.tile([P, 2 * NJ], F32, name="stats")
+
+        vecs = const.tile([P, P], BF16, name="vecs")
+        nc.vector.memset(vecs[:], 0.0)
+        for i, v in enumerate((ba, bx, Lambda)):
+            nc.scalar.dma_start(out=vecs[8 * i:8 * i + 8, :], in_=v.rearrange("o (c p) -> (o c) p", p=P))
+        identb = const.tile([P, P], BF16, name="identb")
+        make_identity(nc, identb[:])
+        ident = const.tile([P, P], F32, name="ident")
+        make_identity(nc, ident[:])
+        zero = const.tile([P, 1], F32, name="zero")
+        nc.vector.memset(zero[:], 0.0)
+        one = const.tile([P, 1], F32, name="one")
+        nc.vector.memset(one[:], 1.0)
+        quarter = const.tile([P, 1], F32, name="quarter")
+        nc.vector.memset(quarter[:], 0.25)
+
+        with ExitStack() as ph1:
+            xraw = ph1.enter_context(tc.tile_pool(name="xraw", bufs=3))
+            hraw = ph1.enter_context(tc.tile_pool(name="hraw", bufs=2))
+            wraw = ph1.enter_context(tc.tile_pool(name="wraw", bufs=W_BUFS))
+            grp = ph1.enter_context(tc.tile_pool(name="grp", bufs=1))
+            xq = ph1.enter_context(tc.tile_pool(name="xq", bufs=2))
+            bl = ph1.enter_context(tc.tile_pool(name="bl", bufs=2))
+            tmp = ph1.enter_context(tc.tile_pool(name="tmp", bufs=4))
+
+            x_tiles = {}
+            h_tiles = {}
+            w_tiles = {}
+            xg_tiles = {}
+            xc_tiles = {}
+            units = {}
+            banks = {}
+
+            def load_x(q, split):
+                xr = xraw.tile([P, 4, D], BF16, name="xr", tag="xr")
+                if split:
+                    for jj in range(4):
+                        nc.sync.dma_start(out=xr[:, jj, :], in_=x_view[:, 4 * q + jj, :])
+                else:
+                    nc.sync.dma_start(out=xr[:], in_=x_view[:, 4 * q:4 * q + 4, :])
+                x_tiles[q] = xr
+
+            def load_h(q):
+                hr = hraw.tile([P, 4, D], BF16, name="hr", tag="hr")
+                nc.sync.dma_start(out=hr[:], in_=h_view[:, 4 * q:4 * q + 4, :])
+                h_tiles[q] = hr
+
+            def load_w(i):
+                wr = wraw.tile([P, D], BF16, name="wr", tag="wr")
+                c = i // 2
+                nc.sync.dma_start(out=wr[:], in_=w_dram[i % 2][c * P:(c + 1) * P, :])
+                w_tiles[i] = wr
+
+            def turn(rows_bf16):
+                words = rows_bf16.bitcast(F32)
+                fr = psum.tile([P, 2, 2, P], F32, name="fr", tag="tp", bufs=TP_BUFS)
+                for g in range(2):
+                    for u in range(2):
+                        nc.tensor.transpose(fr[:, g, u, :], words[:, 256 * g + u:256 * (g + 1):2], ident[:])
+                return fr[:].rearrange("p g u r -> p g r u")
+
+            def fx_turn(q, jj):
+                if jj == 0:
+                    xg_tiles[q] = grp.tile([P, 2, 2048], BF16, name="xg", tag="xg", bufs=1, align_bytes=64)
+                banks[("fx", q, jj)] = turn(x_tiles[q][:, jj, :])
+
+            def fx_copy(q, jj, eng):
+                xgw = xg_tiles[q][:].bitcast(F32)
+                dst = xgw[:, :, jj * 256:(jj + 1) * 256].rearrange("p g (r u) -> p g r u", u=2)
+                if eng == "s":
+                    nc.scalar.copy(out=dst, in_=banks[("fx", q, jj)])
+                else:
+                    nc.vector.tensor_copy(out=dst, in_=banks[("fx", q, jj)])
+
+            def fx_quant(q):
+                xg = xg_tiles[q]
+                xc = xq.tile([P, 2, 512], U32, name="xc", tag="xc", bufs=2, align_bytes=64)
+                xs = xq.tile([P, 2, 512], U8, name="xs", tag="xs", bufs=2, align_bytes=64)
+                for g in range(2):
+                    nc.vector.quantize_mx(out=xc[:, g, :].bitcast(FP8X4), scales=xs[:, g, :], in_=xg[:, g, :])
+                xc_tiles[q] = (xc, xs)
+
+            def fw_turn(i):
+                banks[("fw", i)] = turn(w_tiles[i][:])
+                if i + W_BUFS < 2 * NC:
+                    load_w(i + W_BUFS)
+                if i == 2 * NC - W_BUFS - 1:
+                    load_h(0)
+                    load_x(1, False)
+                    load_h(1)
+                    load_x(2, False)
+
+            def fw_copy(i):
+                wg = grp.tile([P, 2, 512], BF16, name="wg", tag="wg", bufs=3, align_bytes=64)
+                dst = wg[:].bitcast(F32).rearrange("p g (r u) -> p g r u", u=2)
+                if i in W_ON_S:
+                    nc.scalar.copy(out=dst, in_=banks[("fw", i)])
+                else:
+                    nc.vector.tensor_copy(out=dst, in_=banks[("fw", i)])
+                banks[("wg", i)] = wg
+
+            def fw_quant(i):
+                slot = (i % 2) * NC + i // 2
+                nc.vector.quantize_mx(
+                    out=w_codes[:, slot, :].bitcast(FP8X4),
+                    scales=w_scales[:, slot, :],
+                    in_=banks[("wg", i)][:].rearrange("p g n -> p (g n)"),
+                )
+
+            def mxp(s):
+                q = s // 8
+                c = s % 8
+                xc, xs = xc_tiles[q]
+                for gate in range(2):
+                    slot = gate * NC + c
+                    acc = psum.tile([P, 512], F32, name="acc", tag="mx", bufs=MX_BUFS)
+                    for g in range(2):
+                        nc.tensor.matmul_mx(
+                            out=acc[:],
+                            lhsT=w_codes[:, slot, g * P:(g + 1) * P].bitcast(FP8X4),
+                            lhsT_scale=w_scales[:, slot, g * P:(g + 1) * P],
+                            rhs=xc[:, g, :].bitcast(FP8X4),
+                            rhs_scale=xs[:, g, :],
+                            start=(g == 0),
+                            stop=(g == 1),
+                        )
+                    banks[("mx", s, gate)] = acc
+
+            def gate_slot(s, square_on_s):
+                n = s // 4
+                cc = s % 4
+                c = s % 8
+                if cc == 0:
+                    ta = bl.tile([P, 4, 4, P], F32, name="ta", tag="ta", bufs=2)
+                    tx = bl.tile([P, 4, 4, P], F32, name="tx", tag="tx", bufs=3)
+                    a2 = bl.tile([P, 4, 4, P], F32, name="a2", tag="a2", bufs=3)
+                    units[n] = (ta, tx, a2)
+                ta, tx, a2 = units[n]
+                for gate, dst in ((0, ta), (1, tx)):
+                    nc.scalar.activation(
+                        out=dst[:, :, cc, :],
+                        in_=banks[("mx", s, gate)][:].rearrange("p (j r) -> p j r", j=4),
+                        func=ACT.Tanh,
+                        scale=0.5,
+                        bias=hb[:, gate * NC + c:gate * NC + c + 1],
+                    )
+                nc.scalar.activation(out=ta[:, :, cc, :], in_=ta[:, :, cc, :], func=ACT.Exp,
+                                     scale=nhc[:, c:c + 1], bias=nhc[:, c:c + 1])
+                if not square_on_s:
+                    nc.gpsimd.tensor_tensor(out=a2[:, :, cc, :], in0=ta[:, :, cc, :], in1=ta[:, :, cc, :], op=ALU.mult)
+                else:
+                    nc.scalar.activation(out=a2[:, :, cc, :], in_=ta[:, :, cc, :], func=ACT.Square)
+
+            def back(src, jj):
+                bk = psum.tile([P, 512], F32, name="bk", tag="tp", bufs=TP_BUFS)
+                for cc in range(4):
+                    nc.tensor.transpose(bk[:, cc * P:(cc + 1) * P], src[:, jj, cc, :], ident[:])
+                return bk
+
+            def keep_prod(n, jj, bk):
+                q = n // 2
+                G = n % 2
+                nc.vector.tensor_tensor(out=out_sb[:, 4 * q + jj, G * 512:(G + 1) * 512], in0=bk[:],
+                                        in1=h_tiles[q][:, jj, G * 512:(G + 1) * 512], op=ALU.mult)
+
+            def root(n):
+                f = units[n][2][:].rearrange("p j c r -> p (j c r)")
+                nc.scalar.activation(out=f, in_=f, func=ACT.Sqrt, scale=-0.25, bias=quarter[:, 0:1])
+
+            def gmul(t):
+                n = t // 4
+                jj = t % 4
+                tx, a2 = units[n][1:3]
+                f = a2[:, jj].rearrange("p c r -> p (c r)")
+                nc.vector.scalar_tensor_tensor(out=f, in0=tx[:, jj].rearrange("p c r -> p (c r)"), scalar=1.0,
+                                               in1=f, op0=ALU.add, op1=ALU.mult)
+
+            def new_prod(n, jj, bk, add_eng):
+                q = n // 2
+                G = n % 2
+                bt = tmp.tile([P, 512], F32, name="bt", tag="bt", bufs=4)
+                nc.vector.tensor_tensor(out=bt[:], in0=bk[:], in1=x_tiles[q][:, jj, G * 512:(G + 1) * 512], op=ALU.mult)
+                o = out_sb[:, 4 * q + jj, G * 512:(G + 1) * 512]
+                if add_eng == "g":
+                    nc.gpsimd.tensor_tensor(out=o, in0=o, in1=bt[:], op=ALU.add)
+                else:
+                    nc.vector.tensor_tensor(out=o, in0=o, in1=bt[:], op=ALU.add)
+
+            def reduce_bank(t):
+                n = t // 4
+                jj = t % 4
+                q = n // 2
+                G = n % 2
+                nc.vector.tensor_reduce(out=stats[:, t:t + 1], in_=out_sb[:, 4 * q + jj, G * 512:(G + 1) * 512],
+                                        axis=AX.X, op=ALU.max, apply_absolute_value=True)
+                if G == 1:
+                    nc.sync.dma_start(out=o0_view[:, 4 * q + jj, :], in_=out_sb[:, 4 * q + jj, :])
+
+            load_x(0, True)
+            for i in range(W_BUFS):
+                load_w(i)
+            vps = psum.tile([P, P], BF16, name="vps", tag="tp", bufs=TP_BUFS)
+            nc.tensor.transpose(vps[:], vecs[:], identb[:])
+            cols = const.tile([P, 24], F32, name="cols")
+            nc.vector.tensor_copy(out=cols[:], in_=vps[:, 0:24])
+            hb = const.tile([P, 16], F32, name="hb")
+            nc.vector.tensor_scalar(out=hb[:], in0=cols[:, 0:16], scalar1=0.5, scalar2=None, op0=ALU.mult)
+            lam = cols[:, 16:24]
+            sp_a = const.tile([P, NC], F32, name="sp_a")
+            nc.scalar.activation(out=sp_a[:], in_=lam, func=ACT.Abs)
+            sp_e = const.tile([P, NC], F32, name="sp_e")
+            nc.scalar.activation(out=sp_e[:], in_=sp_a[:], func=ACT.Exp, scale=-1.0)
+            sp_l = const.tile([P, NC], F32, name="sp_l")
+            nc.scalar.activation(out=sp_l[:], in_=sp_e[:], func=ACT.Ln, bias=one[:, 0:1])
+            for jj in range(4):
+                fx_turn(0, jj)
+                fx_copy(0, jj, "v")
+            fx_quant(0)
+            sp = const.tile([P, NC], F32, name="sp")
+            nc.vector.scalar_tensor_tensor(out=sp[:], in0=lam, scalar=0.0, in1=sp_l[:], op0=ALU.max, op1=ALU.add)
+            nhc = const.tile([P, NC], F32, name="nhc")
+            nc.vector.tensor_scalar(out=nhc[:], in0=sp[:], scalar1=-4.0, scalar2=None, op0=ALU.mult)
+            for i in range(4):
+                fw_turn(i)
+                fw_copy(i)
+                fw_quant(i)
+            mxp(0)
+
+            jobs = []
+            staged = []
+            prepped = set()
+            added = []
+            bank = {"credit": 0.0}
+
+            def prep(k):
+                for job in [job for job in jobs if job[0] == "g"][0:k]:
+                    if job not in prepped:
+                        prepped.add(job)
+                        gmul(4 * job[1] + job[2])
+
+            def product(last):
+                kind, n, jj, bk = staged.pop(0)
+                q = n // 2
+                if kind == "a":
+                    keep_prod(n, jj, bk)
+                    if n % 2 == 1 and jj == 3 and q + 2 < NQ:
+                        load_h(q + 2)
+                else:
+                    new_prod(n, jj, bk, "v" if last else "g")
+                    if n % 2 == 1 and jj == 3 and q + 3 < NQ:
+                        load_x(q + 3, False)
+                    added.append(4 * n + jj)
+                    if len(added) > RD_LAG:
+                        reduce_bank(added.pop(0))
+
+            def emit_jobs(kind, k):
+                for job in [job for job in jobs if job[0] == kind][0:k]:
+                    if kind == "g":
+                        prep(1)
+                    jobs.remove(job)
+                    staged.append(job + (back(units[job[1]][0 if kind == "a" else 2], job[2]),))
+                    if kind == "g":
+                        prep(LOOK)
+                    if len(staged) > DEPTH:
+                        product(False)
+
+            run_of = {}
+            for run in RUNS:
+                run_of[run[-1]] = run
+
+            for s in range(32):
+                q = s // 8
+                i = s % 8
+                n = s // 4
+                window = (s % 4 == 3) and (n in run_of)
+                if i < 7:
+                    mxp(s + 1)
+                if q == 0 and s + 2 < 8:
+                    for w in (2 * (s + 2), 2 * (s + 2) + 1):
+                        fw_turn(w)
+                if FX_AT[q] <= i < FX_AT[q] + 4 and q + 1 < NQ:
+                    fx_turn(q + 1, i - FX_AT[q])
+                gate_slot(s, window or not SQ_ON_G)
+                if q == 0 and s + 2 < 8:
+                    for w in (2 * (s + 2), 2 * (s + 2) + 1):
+                        fw_copy(w)
+                        fw_quant(w)
+                if FX_AT[q] <= i < FX_AT[q] + 4 and q + 1 < NQ:
+                    fx_copy(q + 1, i - FX_AT[q], "s")
+                    if i == FX_AT[q] + 3:
+                        fx_quant(q + 1)
+                if i == 7 and q + 1 < NQ:
+                    mxp(s + 1)
+                if s % 4 == 3:
+                    for jj in range(4):
+                        jobs.append(("a", n, jj))
+                if window:
+                    for u in run_of[n]:
+                        root(u)
+                    for u in run_of[n]:
+                        for jj in range(4):
+                            jobs.append(("g", u, jj))
+                    emit_jobs("a", 8)
+                    emit_jobs("g", G_PER_WINDOW)
+                    prep(LOOK)
+                else:
+                    emit_jobs("g", 1)
+            emit_jobs("a", 8)
+            emit_jobs("g", 32)
+            while staged:
+                product(len(staged) <= LAST_V)
+            while added:
+                reduce_bank(added.pop(0))
+
+        pm = const.tile([P, 1], F32, name="pm")
+        nc.vector.tensor_reduce(out=pm[:], in_=stats[:], axis=AX.X, op=ALU.max)
+        tp = psum.tile([P, P], F32, name="tp", tag="tp", bufs=TP_BUFS)
+        nc.tensor.transpose(tp[:], pm[:, 0:1].to_broadcast([P, P]), ident[:])
+        am = const.tile([P, 1], F32, name="am")
+        nc.vector.tensor_reduce(out=am[:], in_=tp[:], axis=AX.X, op=ALU.max)
+        rc = const.tile([P, 1], F32, name="rc")
+        nc.vector.reciprocal(out=rc[:], in_=am[:])
+        fac = const.tile([P, 1], F32, name="fac")
+        nc.vector.tensor_scalar(out=fac[:], in0=rc[:], scalar1=448.0, scalar2=None, op0=ALU.mult)
+
+        p2 = ctx.enter_context(tc.tile_pool(name="p2", bufs=4))
+        flat = out_sb[:].rearrange("p j c -> p (j c)")
+        for q in range(NQ):
+            lo = q * 4096
+            o8 = p2.tile([P, 4096], FP8, name="o8", tag="o8", bufs=4)
+            nc.vector.tensor_scalar(out=o8[:, 0:VS], in0=flat[:, lo:lo + VS], scalar1=fac[:, 0:1], scalar2=None,
+                                    op0=ALU.mult, saturate=False)
+            nc.scalar.activation(out=o8[:, VS:4096], in_=flat[:, lo + VS:lo + 4096], func=ACT.Identity,
+                                 scale=fac[:, 0:1], bias=zero[:, 0:1], saturate=False)
+            nc.sync.dma_start(out=o1_view[:, lo:lo + 4096], in_=o8[:].bitcast(U8))

@@ -22,18 +22,16 @@ NJ = B // P
 NQ = 4
 NC = D // P
 VS = 2752
-SQ_ON_G = True
-RD_LAG = 3
 MX_BUFS = 4
 TP_BUFS = 4
-RUNS = ((0,), (1, 2), (3, 4), (5,), (6,), (7,))
-G_PER_WINDOW = 0
-LOOK = 2
-DEPTH = 1
-LAST_V = 1
+RUNS = ((0, 1), (2, 3), (4, 5), (6, 7))
 FX_AT = (4, 2, 2, 2)
 W_BUFS = 8
 W_ON_S = (1, 3, 5, 7)
+X_ON_S = True
+EARLY_PER_SLOT = 2
+LATE_PER_SLOT = 1
+IX_BUFS = 10
 
 
 def tile_cell_kernel(tc, xt, ht_minus_1, Wa, Wx, ba, bx, Lambda, out_0, out_1):
@@ -48,12 +46,16 @@ def tile_cell_kernel(tc, xt, ht_minus_1, Wa, Wx, ba, bx, Lambda, out_0, out_1):
         ctx.enter_context(tc.manual_schedule(engines={mybir.EngineType.Activation}))
         const = ctx.enter_context(tc.tile_pool(name="const", bufs=1))
         keep = ctx.enter_context(tc.tile_pool(name="keep", bufs=1))
+        share = ctx.enter_context(tc.tile_pool(name="share", bufs=1))
         psum = ctx.enter_context(tc.psum_pool(name="psum", bufs=2))
 
-        out_sb = keep.tile([P, NJ, D], F32, name="out_sb")
         w_codes = keep.tile([P, 2 * NC, 256], U32, name="w_codes", align_bytes=64)
         w_scales = keep.tile([P, 2 * NC, 256], U8, name="w_scales", align_bytes=64)
         stats = const.tile([P, 2 * NJ], F32, name="stats")
+        outs = []
+        for q in range(NQ - 1):
+            o_q = keep.tile([P, 4, D], F32, name="o_q%d" % q)
+            outs.append(o_q)
 
         vecs = const.tile([P, P], BF16, name="vecs")
         nc.vector.memset(vecs[:], 0.0)
@@ -73,7 +75,6 @@ def tile_cell_kernel(tc, xt, ht_minus_1, Wa, Wx, ba, bx, Lambda, out_0, out_1):
         with ExitStack() as ph1:
             xraw = ph1.enter_context(tc.tile_pool(name="xraw", bufs=3))
             hraw = ph1.enter_context(tc.tile_pool(name="hraw", bufs=2))
-            wraw = ph1.enter_context(tc.tile_pool(name="wraw", bufs=W_BUFS))
             grp = ph1.enter_context(tc.tile_pool(name="grp", bufs=1))
             xq = ph1.enter_context(tc.tile_pool(name="xq", bufs=2))
             bl = ph1.enter_context(tc.tile_pool(name="bl", bufs=2))
@@ -102,7 +103,7 @@ def tile_cell_kernel(tc, xt, ht_minus_1, Wa, Wx, ba, bx, Lambda, out_0, out_1):
                 h_tiles[q] = hr
 
             def load_w(i):
-                wr = wraw.tile([P, D], BF16, name="wr", tag="wr")
+                wr = share.tile([P, D], BF16, name="wr", tag="wr", bufs=W_BUFS, offset=0)
                 c = i // 2
                 nc.sync.dma_start(out=wr[:], in_=w_dram[i % 2][c * P:(c + 1) * P, :])
                 w_tiles[i] = wr
@@ -120,10 +121,10 @@ def tile_cell_kernel(tc, xt, ht_minus_1, Wa, Wx, ba, bx, Lambda, out_0, out_1):
                     xg_tiles[q] = grp.tile([P, 2, 2048], BF16, name="xg", tag="xg", bufs=1, align_bytes=64)
                 banks[("fx", q, jj)] = turn(x_tiles[q][:, jj, :])
 
-            def fx_copy(q, jj, eng):
+            def fx_copy(q, jj, on_s):
                 xgw = xg_tiles[q][:].bitcast(F32)
                 dst = xgw[:, :, jj * 256:(jj + 1) * 256].rearrange("p g (r u) -> p g r u", u=2)
-                if eng == "s":
+                if on_s:
                     nc.scalar.copy(out=dst, in_=banks[("fx", q, jj)])
                 else:
                     nc.vector.tensor_copy(out=dst, in_=banks[("fx", q, jj)])
@@ -147,7 +148,7 @@ def tile_cell_kernel(tc, xt, ht_minus_1, Wa, Wx, ba, bx, Lambda, out_0, out_1):
                     load_x(2, False)
 
             def fw_copy(i):
-                wg = grp.tile([P, 2, 512], BF16, name="wg", tag="wg", bufs=3, align_bytes=64)
+                wg = grp.tile([P, 2, 512], BF16, name="wg", tag="wg", bufs=2, align_bytes=64)
                 dst = wg[:].bitcast(F32).rearrange("p g (r u) -> p g r u", u=2)
                 if i in W_ON_S:
                     nc.scalar.copy(out=dst, in_=banks[("fw", i)])
@@ -182,13 +183,13 @@ def tile_cell_kernel(tc, xt, ht_minus_1, Wa, Wx, ba, bx, Lambda, out_0, out_1):
                         )
                     banks[("mx", s, gate)] = acc
 
-            def gate_slot(s, square_on_s):
+            def gate_slot(s):
                 n = s // 4
                 cc = s % 4
                 c = s % 8
                 if cc == 0:
                     ta = bl.tile([P, 4, 4, P], F32, name="ta", tag="ta", bufs=2)
-                    tx = bl.tile([P, 4, 4, P], F32, name="tx", tag="tx", bufs=3)
+                    tx = bl.tile([P, 4, 4, P], F32, name="tx", tag="tx", bufs=2)
                     a2 = bl.tile([P, 4, 4, P], F32, name="a2", tag="a2", bufs=3)
                     units[n] = (ta, tx, a2)
                 ta, tx, a2 = units[n]
@@ -202,10 +203,7 @@ def tile_cell_kernel(tc, xt, ht_minus_1, Wa, Wx, ba, bx, Lambda, out_0, out_1):
                     )
                 nc.scalar.activation(out=ta[:, :, cc, :], in_=ta[:, :, cc, :], func=ACT.Exp,
                                      scale=nhc[:, c:c + 1], bias=nhc[:, c:c + 1])
-                if not square_on_s:
-                    nc.gpsimd.tensor_tensor(out=a2[:, :, cc, :], in0=ta[:, :, cc, :], in1=ta[:, :, cc, :], op=ALU.mult)
-                else:
-                    nc.scalar.activation(out=a2[:, :, cc, :], in_=ta[:, :, cc, :], func=ACT.Square)
+                nc.gpsimd.tensor_tensor(out=a2[:, :, cc, :], in0=ta[:, :, cc, :], in1=ta[:, :, cc, :], op=ALU.mult)
 
             def back(src, jj):
                 bk = psum.tile([P, 512], F32, name="bk", tag="tp", bufs=TP_BUFS)
@@ -213,44 +211,41 @@ def tile_cell_kernel(tc, xt, ht_minus_1, Wa, Wx, ba, bx, Lambda, out_0, out_1):
                     nc.tensor.transpose(bk[:, cc * P:(cc + 1) * P], src[:, jj, cc, :], ident[:])
                 return bk
 
-            def keep_prod(n, jj, bk):
-                q = n // 2
-                G = n % 2
-                nc.vector.tensor_tensor(out=out_sb[:, 4 * q + jj, G * 512:(G + 1) * 512], in0=bk[:],
-                                        in1=h_tiles[q][:, jj, G * 512:(G + 1) * 512], op=ALU.mult)
-
             def root(n):
                 f = units[n][2][:].rearrange("p j c r -> p (j c r)")
                 nc.scalar.activation(out=f, in_=f, func=ACT.Sqrt, scale=-0.25, bias=quarter[:, 0:1])
 
-            def gmul(t):
-                n = t // 4
-                jj = t % 4
-                tx, a2 = units[n][1:3]
-                f = a2[:, jj].rearrange("p c r -> p (c r)")
-                nc.vector.scalar_tensor_tensor(out=f, in0=tx[:, jj].rearrange("p c r -> p (c r)"), scalar=1.0,
-                                               in1=f, op0=ALU.add, op1=ALU.mult)
-
-            def new_prod(n, jj, bk, add_eng):
+            def do_job(job):
+                kind, n, jj = job
                 q = n // 2
-                G = n % 2
-                bt = tmp.tile([P, 512], F32, name="bt", tag="bt", bufs=4)
-                nc.vector.tensor_tensor(out=bt[:], in0=bk[:], in1=x_tiles[q][:, jj, G * 512:(G + 1) * 512], op=ALU.mult)
-                o = out_sb[:, 4 * q + jj, G * 512:(G + 1) * 512]
-                if add_eng == "g":
-                    nc.gpsimd.tensor_tensor(out=o, in0=o, in1=bt[:], op=ALU.add)
+                half = slice((n % 2) * 512, (n % 2) * 512 + 512)
+                if q == NQ - 1 and len(outs) < NQ:
+                    o_last = share.tile([P, 4, D], F32, name="o_last", offset=0)
+                    outs.append(o_last)
+                o = outs[q][:, jj, half]
+                if kind == "a":
+                    bk = back(units[n][0], jj)
+                    nc.vector.tensor_tensor(out=o, in0=bk[:], in1=h_tiles[q][:, jj, half], op=ALU.mult)
+                    if n % 2 == 1 and jj == 3 and q + 2 < NQ:
+                        load_h(q + 2)
+                elif kind == "x":
+                    bk = back(units[n][1], jj)
+                    ix = tmp.tile([P, 512], F32, name="ix", tag="ix", bufs=IX_BUFS)
+                    nc.vector.scalar_tensor_tensor(out=ix[:], in0=bk[:], scalar=1.0, in1=x_tiles[q][:, jj, half],
+                                                   op0=ALU.add, op1=ALU.mult)
+                    banks[("ix", n, jj)] = ix
+                    if n % 2 == 1 and jj == 3 and q + 3 < NQ:
+                        load_x(q + 3, False)
                 else:
-                    nc.vector.tensor_tensor(out=o, in0=o, in1=bt[:], op=ALU.add)
-
-            def reduce_bank(t):
-                n = t // 4
-                jj = t % 4
-                q = n // 2
-                G = n % 2
-                nc.vector.tensor_reduce(out=stats[:, t:t + 1], in_=out_sb[:, 4 * q + jj, G * 512:(G + 1) * 512],
-                                        axis=AX.X, op=ALU.max, apply_absolute_value=True)
-                if G == 1:
-                    nc.sync.dma_start(out=o0_view[:, 4 * q + jj, :], in_=out_sb[:, 4 * q + jj, :])
+                    bk = back(units[n][2], jj)
+                    bt = tmp.tile([P, 512], F32, name="bt", tag="bt", bufs=3)
+                    nc.vector.tensor_tensor(out=bt[:], in0=bk[:], in1=banks[("ix", n, jj)][:], op=ALU.mult)
+                    nc.gpsimd.tensor_tensor(out=o, in0=o, in1=bt[:], op=ALU.add)
+                    t = 4 * n + jj
+                    nc.vector.tensor_reduce(out=stats[:, t:t + 1], in_=o, axis=AX.X, op=ALU.max,
+                                            apply_absolute_value=True)
+                    if n % 2 == 1:
+                        nc.sync.dma_start(out=o0_view[:, 4 * q + jj, :], in_=outs[q][:, jj, :])
 
             load_x(0, True)
             for i in range(W_BUFS):
@@ -270,7 +265,7 @@ def tile_cell_kernel(tc, xt, ht_minus_1, Wa, Wx, ba, bx, Lambda, out_0, out_1):
             nc.scalar.activation(out=sp_l[:], in_=sp_e[:], func=ACT.Ln, bias=one[:, 0:1])
             for jj in range(4):
                 fx_turn(0, jj)
-                fx_copy(0, jj, "v")
+                fx_copy(0, jj, False)
             fx_quant(0)
             sp = const.tile([P, NC], F32, name="sp")
             nc.vector.scalar_tensor_tensor(out=sp[:], in0=lam, scalar=0.0, in1=sp_l[:], op0=ALU.max, op1=ALU.add)
@@ -282,43 +277,12 @@ def tile_cell_kernel(tc, xt, ht_minus_1, Wa, Wx, ba, bx, Lambda, out_0, out_1):
                 fw_quant(i)
             mxp(0)
 
-            jobs = []
-            staged = []
-            prepped = set()
-            added = []
-            bank = {"credit": 0.0}
+            early = []
+            late = []
 
-            def prep(k):
-                for job in [job for job in jobs if job[0] == "g"][0:k]:
-                    if job not in prepped:
-                        prepped.add(job)
-                        gmul(4 * job[1] + job[2])
-
-            def product(last):
-                kind, n, jj, bk = staged.pop(0)
-                q = n // 2
-                if kind == "a":
-                    keep_prod(n, jj, bk)
-                    if n % 2 == 1 and jj == 3 and q + 2 < NQ:
-                        load_h(q + 2)
-                else:
-                    new_prod(n, jj, bk, "v" if last else "g")
-                    if n % 2 == 1 and jj == 3 and q + 3 < NQ:
-                        load_x(q + 3, False)
-                    added.append(4 * n + jj)
-                    if len(added) > RD_LAG:
-                        reduce_bank(added.pop(0))
-
-            def emit_jobs(kind, k):
-                for job in [job for job in jobs if job[0] == kind][0:k]:
-                    if kind == "g":
-                        prep(1)
-                    jobs.remove(job)
-                    staged.append(job + (back(units[job[1]][0 if kind == "a" else 2], job[2]),))
-                    if kind == "g":
-                        prep(LOOK)
-                    if len(staged) > DEPTH:
-                        product(False)
+            def emit(queue, k):
+                for r in range(min(k, len(queue))):
+                    do_job(queue.pop(0))
 
             run_of = {}
             for run in RUNS:
@@ -334,39 +298,34 @@ def tile_cell_kernel(tc, xt, ht_minus_1, Wa, Wx, ba, bx, Lambda, out_0, out_1):
                 if q == 0 and s + 2 < 8:
                     for w in (2 * (s + 2), 2 * (s + 2) + 1):
                         fw_turn(w)
-                if FX_AT[q] <= i < FX_AT[q] + 4 and q + 1 < NQ:
+                fx_now = FX_AT[q] <= i < FX_AT[q] + 4 and q + 1 < NQ
+                if fx_now:
                     fx_turn(q + 1, i - FX_AT[q])
-                gate_slot(s, window or not SQ_ON_G)
+                gate_slot(s)
                 if q == 0 and s + 2 < 8:
                     for w in (2 * (s + 2), 2 * (s + 2) + 1):
                         fw_copy(w)
                         fw_quant(w)
-                if FX_AT[q] <= i < FX_AT[q] + 4 and q + 1 < NQ:
-                    fx_copy(q + 1, i - FX_AT[q], "s")
+                if fx_now:
+                    fx_copy(q + 1, i - FX_AT[q], X_ON_S)
                     if i == FX_AT[q] + 3:
                         fx_quant(q + 1)
                 if i == 7 and q + 1 < NQ:
                     mxp(s + 1)
                 if s % 4 == 3:
                     for jj in range(4):
-                        jobs.append(("a", n, jj))
+                        early.append(("a", n, jj))
+                        early.append(("x", n, jj))
+                emit(late, LATE_PER_SLOT)
+                emit(early, EARLY_PER_SLOT)
                 if window:
                     for u in run_of[n]:
                         root(u)
                     for u in run_of[n]:
                         for jj in range(4):
-                            jobs.append(("g", u, jj))
-                    emit_jobs("a", 8)
-                    emit_jobs("g", G_PER_WINDOW)
-                    prep(LOOK)
-                else:
-                    emit_jobs("g", 1)
-            emit_jobs("a", 8)
-            emit_jobs("g", 32)
-            while staged:
-                product(len(staged) <= LAST_V)
-            while added:
-                reduce_bank(added.pop(0))
+                            late.append(("s", u, jj))
+            emit(early, len(early))
+            emit(late, len(late))
 
         pm = const.tile([P, 1], F32, name="pm")
         nc.vector.tensor_reduce(out=pm[:], in_=stats[:], axis=AX.X, op=ALU.max)
@@ -380,12 +339,12 @@ def tile_cell_kernel(tc, xt, ht_minus_1, Wa, Wx, ba, bx, Lambda, out_0, out_1):
         nc.vector.tensor_scalar(out=fac[:], in0=rc[:], scalar1=448.0, scalar2=None, op0=ALU.mult)
 
         p2 = ctx.enter_context(tc.tile_pool(name="p2", bufs=4))
-        flat = out_sb[:].rearrange("p j c -> p (j c)")
         for q in range(NQ):
             lo = q * 4096
+            flat = outs[q][:].rearrange("p j c -> p (j c)")
             o8 = p2.tile([P, 4096], FP8, name="o8", tag="o8", bufs=4)
-            nc.vector.tensor_scalar(out=o8[:, 0:VS], in0=flat[:, lo:lo + VS], scalar1=fac[:, 0:1], scalar2=None,
+            nc.vector.tensor_scalar(out=o8[:, 0:VS], in0=flat[:, 0:VS], scalar1=fac[:, 0:1], scalar2=None,
                                     op0=ALU.mult, saturate=False)
-            nc.scalar.activation(out=o8[:, VS:4096], in_=flat[:, lo + VS:lo + 4096], func=ACT.Identity,
+            nc.scalar.activation(out=o8[:, VS:4096], in_=flat[:, VS:4096], func=ACT.Identity,
                                  scale=fac[:, 0:1], bias=zero[:, 0:1], saturate=False)
             nc.sync.dma_start(out=o1_view[:, lo:lo + 4096], in_=o8[:].bitcast(U8))

@@ -26,12 +26,21 @@ MX_BUFS = 4
 TP_BUFS = 4
 RUNS = ((0, 1), (2, 3), (4, 5), (6, 7))
 FX_AT = (4, 2, 2, 2)
-W_BUFS = 8
+W_BUFS = 16
 W_ON_S = (1, 3, 5, 7)
-X_ON_S = True
+X_ON_S = (0, 2)
+TAIL_ON_V = (0, 3, 6)
+WIDE_RD = 3
 EARLY_PER_SLOT = 2
 LATE_PER_SLOT = 1
 IX_BUFS = 10
+RD_LAG = 3
+SQ_LAST_ON_S = True
+H0_AFTER = 8
+X1_AFTER = 12
+TAIL_LAG = 1
+EARLY_IN_WINDOW = 6
+LATE_IN_WINDOW = 4
 
 
 def tile_cell_kernel(tc, xt, ht_minus_1, Wa, Wx, ba, bx, Lambda, out_0, out_1):
@@ -43,7 +52,7 @@ def tile_cell_kernel(tc, xt, ht_minus_1, Wa, Wx, ba, bx, Lambda, out_0, out_1):
     w_dram = (Wa, Wx)
 
     with ExitStack() as ctx:
-        ctx.enter_context(tc.manual_schedule(engines={mybir.EngineType.Activation}))
+        ctx.enter_context(tc.manual_schedule())
         const = ctx.enter_context(tc.tile_pool(name="const", bufs=1))
         keep = ctx.enter_context(tc.tile_pool(name="keep", bufs=1))
         share = ctx.enter_context(tc.tile_pool(name="share", bufs=1))
@@ -52,8 +61,9 @@ def tile_cell_kernel(tc, xt, ht_minus_1, Wa, Wx, ba, bx, Lambda, out_0, out_1):
         w_codes = keep.tile([P, 2 * NC, 256], U32, name="w_codes", align_bytes=64)
         w_scales = keep.tile([P, 2 * NC, 256], U8, name="w_scales", align_bytes=64)
         stats = const.tile([P, 2 * NJ], F32, name="stats")
+        nc.vector.memset(stats[:], 0.0)
         outs = []
-        for q in range(NQ - 1):
+        for q in range(NQ - 2):
             o_q = keep.tile([P, 4, D], F32, name="o_q%d" % q)
             outs.append(o_q)
 
@@ -139,13 +149,6 @@ def tile_cell_kernel(tc, xt, ht_minus_1, Wa, Wx, ba, bx, Lambda, out_0, out_1):
 
             def fw_turn(i):
                 banks[("fw", i)] = turn(w_tiles[i][:])
-                if i + W_BUFS < 2 * NC:
-                    load_w(i + W_BUFS)
-                if i == 2 * NC - W_BUFS - 1:
-                    load_h(0)
-                    load_x(1, False)
-                    load_h(1)
-                    load_x(2, False)
 
             def fw_copy(i):
                 wg = grp.tile([P, 2, 512], BF16, name="wg", tag="wg", bufs=2, align_bytes=64)
@@ -183,7 +186,7 @@ def tile_cell_kernel(tc, xt, ht_minus_1, Wa, Wx, ba, bx, Lambda, out_0, out_1):
                         )
                     banks[("mx", s, gate)] = acc
 
-            def gate_slot(s):
+            def gate_slot(s, square_on_s):
                 n = s // 4
                 cc = s % 4
                 c = s % 8
@@ -203,7 +206,10 @@ def tile_cell_kernel(tc, xt, ht_minus_1, Wa, Wx, ba, bx, Lambda, out_0, out_1):
                     )
                 nc.scalar.activation(out=ta[:, :, cc, :], in_=ta[:, :, cc, :], func=ACT.Exp,
                                      scale=nhc[:, c:c + 1], bias=nhc[:, c:c + 1])
-                nc.gpsimd.tensor_tensor(out=a2[:, :, cc, :], in0=ta[:, :, cc, :], in1=ta[:, :, cc, :], op=ALU.mult)
+                if square_on_s:
+                    nc.scalar.activation(out=a2[:, :, cc, :], in_=ta[:, :, cc, :], func=ACT.Square)
+                else:
+                    nc.gpsimd.tensor_tensor(out=a2[:, :, cc, :], in0=ta[:, :, cc, :], in1=ta[:, :, cc, :], op=ALU.mult)
 
             def back(src, jj):
                 bk = psum.tile([P, 512], F32, name="bk", tag="tp", bufs=TP_BUFS)
@@ -215,13 +221,13 @@ def tile_cell_kernel(tc, xt, ht_minus_1, Wa, Wx, ba, bx, Lambda, out_0, out_1):
                 f = units[n][2][:].rearrange("p j c r -> p (j c r)")
                 nc.scalar.activation(out=f, in_=f, func=ACT.Sqrt, scale=-0.25, bias=quarter[:, 0:1])
 
-            def do_job(job):
+            def do_job(job, on_v):
                 kind, n, jj = job
                 q = n // 2
                 half = slice((n % 2) * 512, (n % 2) * 512 + 512)
-                if q == NQ - 1 and len(outs) < NQ:
-                    o_last = share.tile([P, 4, D], F32, name="o_last", offset=0)
-                    outs.append(o_last)
+                if q == len(outs):
+                    o_late = share.tile([P, 4, D], F32, name="o_late%d" % q, offset=(q - 2) * 16384)
+                    outs.append(o_late)
                 o = outs[q][:, jj, half]
                 if kind == "a":
                     bk = back(units[n][0], jj)
@@ -240,16 +246,37 @@ def tile_cell_kernel(tc, xt, ht_minus_1, Wa, Wx, ba, bx, Lambda, out_0, out_1):
                     bk = back(units[n][2], jj)
                     bt = tmp.tile([P, 512], F32, name="bt", tag="bt", bufs=3)
                     nc.vector.tensor_tensor(out=bt[:], in0=bk[:], in1=banks[("ix", n, jj)][:], op=ALU.mult)
-                    nc.gpsimd.tensor_tensor(out=o, in0=o, in1=bt[:], op=ALU.add)
-                    t = 4 * n + jj
-                    nc.vector.tensor_reduce(out=stats[:, t:t + 1], in_=o, axis=AX.X, op=ALU.max,
+                    if on_v:
+                        nc.vector.tensor_tensor(out=o, in0=o, in1=bt[:], op=ALU.add)
+                    else:
+                        nc.gpsimd.tensor_tensor(out=o, in0=o, in1=bt[:], op=ALU.add)
+                    pending.append((n, jj))
+
+            def reduce_one():
+                n, jj = pending.pop(0)
+                q = n // 2
+                t = 4 * n + jj
+                half = slice((n % 2) * 512, (n % 2) * 512 + 512)
+                if q >= WIDE_RD:
+                    nc.vector.tensor_reduce(out=stats[:, t:t + 1], in_=outs[q][:, jj, half], axis=AX.X, op=ALU.max,
                                             apply_absolute_value=True)
-                    if n % 2 == 1:
-                        nc.sync.dma_start(out=o0_view[:, 4 * q + jj, :], in_=outs[q][:, jj, :])
+                elif n % 2 == 1:
+                    nc.vector.tensor_reduce(out=stats[:, t:t + 1], in_=outs[q][:, jj, :], axis=AX.X, op=ALU.max,
+                                            apply_absolute_value=True)
+                if n % 2 == 1:
+                    nc.sync.dma_start(out=o0_view[:, 4 * q + jj, :], in_=outs[q][:, jj, :])
+
+            pending = []
 
             load_x(0, True)
             for i in range(W_BUFS):
                 load_w(i)
+                if i + 1 == H0_AFTER:
+                    load_h(0)
+                if i + 1 == X1_AFTER:
+                    load_x(1, False)
+            load_h(1)
+            load_x(2, False)
             vps = psum.tile([P, P], BF16, name="vps", tag="tp", bufs=TP_BUFS)
             nc.tensor.transpose(vps[:], vecs[:], identb[:])
             cols = const.tile([P, 24], F32, name="cols")
@@ -263,6 +290,8 @@ def tile_cell_kernel(tc, xt, ht_minus_1, Wa, Wx, ba, bx, Lambda, out_0, out_1):
             nc.scalar.activation(out=sp_e[:], in_=sp_a[:], func=ACT.Exp, scale=-1.0)
             sp_l = const.tile([P, NC], F32, name="sp_l")
             nc.scalar.activation(out=sp_l[:], in_=sp_e[:], func=ACT.Ln, bias=one[:, 0:1])
+            warm = const.tile([P, 1], F32, name="warm")
+            nc.scalar.activation(out=warm[:], in_=zero[:], func=ACT.Tanh)
             for jj in range(4):
                 fx_turn(0, jj)
                 fx_copy(0, jj, False)
@@ -282,7 +311,9 @@ def tile_cell_kernel(tc, xt, ht_minus_1, Wa, Wx, ba, bx, Lambda, out_0, out_1):
 
             def emit(queue, k):
                 for r in range(min(k, len(queue))):
-                    do_job(queue.pop(0))
+                    do_job(queue.pop(0), False)
+                    if len(pending) > RD_LAG:
+                        reduce_one()
 
             run_of = {}
             for run in RUNS:
@@ -301,13 +332,13 @@ def tile_cell_kernel(tc, xt, ht_minus_1, Wa, Wx, ba, bx, Lambda, out_0, out_1):
                 fx_now = FX_AT[q] <= i < FX_AT[q] + 4 and q + 1 < NQ
                 if fx_now:
                     fx_turn(q + 1, i - FX_AT[q])
-                gate_slot(s)
+                gate_slot(s, window and SQ_LAST_ON_S)
                 if q == 0 and s + 2 < 8:
                     for w in (2 * (s + 2), 2 * (s + 2) + 1):
                         fw_copy(w)
                         fw_quant(w)
                 if fx_now:
-                    fx_copy(q + 1, i - FX_AT[q], X_ON_S)
+                    fx_copy(q + 1, i - FX_AT[q], (i - FX_AT[q]) in X_ON_S)
                     if i == FX_AT[q] + 3:
                         fx_quant(q + 1)
                 if i == 7 and q + 1 < NQ:
@@ -316,16 +347,24 @@ def tile_cell_kernel(tc, xt, ht_minus_1, Wa, Wx, ba, bx, Lambda, out_0, out_1):
                     for jj in range(4):
                         early.append(("a", n, jj))
                         early.append(("x", n, jj))
-                emit(late, LATE_PER_SLOT)
-                emit(early, EARLY_PER_SLOT)
                 if window:
                     for u in run_of[n]:
                         root(u)
+                    emit(early, EARLY_IN_WINDOW)
                     for u in run_of[n]:
                         for jj in range(4):
                             late.append(("s", u, jj))
+                    emit(late, LATE_IN_WINDOW)
+                else:
+                    emit(late, LATE_PER_SLOT)
+                    emit(early, EARLY_PER_SLOT)
             emit(early, len(early))
-            emit(late, len(late))
+            while late:
+                do_job(late.pop(0), len(late) % 8 in TAIL_ON_V)
+                if len(pending) > TAIL_LAG:
+                    reduce_one()
+            while pending:
+                reduce_one()
 
         pm = const.tile([P, 1], F32, name="pm")
         nc.vector.tensor_reduce(out=pm[:], in_=stats[:], axis=AX.X, op=ALU.max)

@@ -27,15 +27,16 @@ TP_BUFS = 4
 RUNS = ((0, 1), (2, 3), (4, 5), (6, 7))
 FX_AT = (4, 2, 2, 2)
 W_BUFS = 16
-W_ON_S = (1, 3, 5, 7)
-X_ON_S = (0, 2)
-TAIL_ON_V = (0, 3, 6)
+W_ON_S = (0, 1, 2, 3)
+X_ON_S = ((), (), (), ())
+TAIL_ON_V = ()
 WIDE_RD = 3
 EARLY_PER_SLOT = 2
 LATE_PER_SLOT = 1
 IX_BUFS = 10
 RD_LAG = 3
-SQ_LAST_ON_S = True
+A2_BUFS = 3
+SQ_LAST_ON_S = False
 H0_AFTER = 8
 X1_AFTER = 12
 TAIL_LAG = 1
@@ -193,7 +194,7 @@ def tile_cell_kernel(tc, xt, ht_minus_1, Wa, Wx, ba, bx, Lambda, out_0, out_1):
                 if cc == 0:
                     ta = bl.tile([P, 4, 4, P], F32, name="ta", tag="ta", bufs=2)
                     tx = bl.tile([P, 4, 4, P], F32, name="tx", tag="tx", bufs=2)
-                    a2 = bl.tile([P, 4, 4, P], F32, name="a2", tag="a2", bufs=3)
+                    a2 = bl.tile([P, 4, 4, P], F32, name="a2", tag="a2", bufs=A2_BUFS)
                     units[n] = (ta, tx, a2)
                 ta, tx, a2 = units[n]
                 for gate, dst in ((0, ta), (1, tx)):
@@ -338,7 +339,7 @@ def tile_cell_kernel(tc, xt, ht_minus_1, Wa, Wx, ba, bx, Lambda, out_0, out_1):
                         fw_copy(w)
                         fw_quant(w)
                 if fx_now:
-                    fx_copy(q + 1, i - FX_AT[q], (i - FX_AT[q]) in X_ON_S)
+                    fx_copy(q + 1, i - FX_AT[q], (i - FX_AT[q]) in X_ON_S[q])
                     if i == FX_AT[q] + 3:
                         fx_quant(q + 1)
                 if i == 7 and q + 1 < NQ:

@@ -21,27 +21,19 @@ D = 1024
 NJ = B // P
 NQ = 4
 NC = D // P
+NSLOT = NQ * NC
 VS = 2752
 MX_BUFS = 4
 TP_BUFS = 4
-RUNS = ((0, 1), (2, 3), (4, 5), (6, 7))
-FX_AT = (4, 2, 2, 2)
-W_BUFS = 16
-W_ON_S = (0, 1, 2, 3)
-X_ON_S = ((), (), (), ())
-TAIL_ON_V = ()
-WIDE_RD = 3
-EARLY_PER_SLOT = 2
-LATE_PER_SLOT = 1
 IX_BUFS = 10
-RD_LAG = 3
-A2_BUFS = 3
-SQ_LAST_ON_S = False
-H0_AFTER = 8
-X1_AFTER = 12
-TAIL_LAG = 1
+FX_AT = (2, 2, 2)
+LATE_PER_SLOT = 1
+EARLY_PER_SLOT = 2
 EARLY_IN_WINDOW = 6
 LATE_IN_WINDOW = 4
+RD_LAG = 4
+H0_AFTER = 8
+X1_AFTER = 12
 
 
 def tile_cell_kernel(tc, xt, ht_minus_1, Wa, Wx, ba, bx, Lambda, out_0, out_1):
@@ -59,12 +51,12 @@ def tile_cell_kernel(tc, xt, ht_minus_1, Wa, Wx, ba, bx, Lambda, out_0, out_1):
         share = ctx.enter_context(tc.tile_pool(name="share", bufs=1))
         psum = ctx.enter_context(tc.psum_pool(name="psum", bufs=2))
 
-        w_codes = keep.tile([P, 2 * NC, 256], U32, name="w_codes", align_bytes=64)
-        w_scales = keep.tile([P, 2 * NC, 256], U8, name="w_scales", align_bytes=64)
-        stats = const.tile([P, 2 * NJ], F32, name="stats")
+        w_codes = keep.tile([P, NC, 2, 256], U32, name="w_codes", align_bytes=64)
+        w_scales = keep.tile([P, NC, 2, 256], U8, name="w_scales", align_bytes=64)
+        stats = const.tile([P, NJ], F32, name="stats")
         nc.vector.memset(stats[:], 0.0)
         outs = []
-        for q in range(NQ - 2):
+        for q in range(2):
             o_q = keep.tile([P, 4, D], F32, name="o_q%d" % q)
             outs.append(o_q)
 
@@ -95,15 +87,16 @@ def tile_cell_kernel(tc, xt, ht_minus_1, Wa, Wx, ba, bx, Lambda, out_0, out_1):
             h_tiles = {}
             w_tiles = {}
             xg_tiles = {}
+            wg_tiles = {}
             xc_tiles = {}
             units = {}
             banks = {}
 
-            def load_x(q, split):
+            def load_x(q):
                 xr = xraw.tile([P, 4, D], BF16, name="xr", tag="xr")
-                if split:
+                if q == 0:
                     for jj in range(4):
-                        nc.sync.dma_start(out=xr[:, jj, :], in_=x_view[:, 4 * q + jj, :])
+                        nc.sync.dma_start(out=xr[:, jj, :], in_=x_view[:, jj, :])
                 else:
                     nc.sync.dma_start(out=xr[:], in_=x_view[:, 4 * q:4 * q + 4, :])
                 x_tiles[q] = xr
@@ -113,11 +106,10 @@ def tile_cell_kernel(tc, xt, ht_minus_1, Wa, Wx, ba, bx, Lambda, out_0, out_1):
                 nc.sync.dma_start(out=hr[:], in_=h_view[:, 4 * q:4 * q + 4, :])
                 h_tiles[q] = hr
 
-            def load_w(i):
-                wr = share.tile([P, D], BF16, name="wr", tag="wr", bufs=W_BUFS, offset=0)
-                c = i // 2
-                nc.sync.dma_start(out=wr[:], in_=w_dram[i % 2][c * P:(c + 1) * P, :])
-                w_tiles[i] = wr
+            def load_w(c, gate):
+                wr = share.tile([P, D], BF16, name="wr", tag="wr", bufs=2 * NC, offset=0)
+                nc.sync.dma_start(out=wr[:], in_=w_dram[gate][c * P:(c + 1) * P, :])
+                w_tiles[(c, gate)] = wr
 
             def turn(rows_bf16):
                 words = rows_bf16.bitcast(F32)
@@ -132,13 +124,13 @@ def tile_cell_kernel(tc, xt, ht_minus_1, Wa, Wx, ba, bx, Lambda, out_0, out_1):
                     xg_tiles[q] = grp.tile([P, 2, 2048], BF16, name="xg", tag="xg", bufs=1, align_bytes=64)
                 banks[("fx", q, jj)] = turn(x_tiles[q][:, jj, :])
 
-            def fx_copy(q, jj, on_s):
+            def fx_copy(q, jj):
                 xgw = xg_tiles[q][:].bitcast(F32)
                 dst = xgw[:, :, jj * 256:(jj + 1) * 256].rearrange("p g (r u) -> p g r u", u=2)
-                if on_s:
-                    nc.scalar.copy(out=dst, in_=banks[("fx", q, jj)])
-                else:
+                if q == 0:
                     nc.vector.tensor_copy(out=dst, in_=banks[("fx", q, jj)])
+                else:
+                    nc.scalar.copy(out=dst, in_=banks[("fx", q, jj)])
 
             def fx_quant(q):
                 xg = xg_tiles[q]
@@ -148,38 +140,35 @@ def tile_cell_kernel(tc, xt, ht_minus_1, Wa, Wx, ba, bx, Lambda, out_0, out_1):
                     nc.vector.quantize_mx(out=xc[:, g, :].bitcast(FP8X4), scales=xs[:, g, :], in_=xg[:, g, :])
                 xc_tiles[q] = (xc, xs)
 
-            def fw_turn(i):
-                banks[("fw", i)] = turn(w_tiles[i][:])
+            def fw_turn(c):
+                for gate in range(2):
+                    banks[("fw", c, gate)] = turn(w_tiles[(c, gate)][:])
 
-            def fw_copy(i):
-                wg = grp.tile([P, 2, 512], BF16, name="wg", tag="wg", bufs=2, align_bytes=64)
-                dst = wg[:].bitcast(F32).rearrange("p g (r u) -> p g r u", u=2)
-                if i in W_ON_S:
-                    nc.scalar.copy(out=dst, in_=banks[("fw", i)])
-                else:
-                    nc.vector.tensor_copy(out=dst, in_=banks[("fw", i)])
-                banks[("wg", i)] = wg
-
-            def fw_quant(i):
-                slot = (i % 2) * NC + i // 2
+            def fw_finish(c):
+                wg = grp.tile([P, 2, 2, 512], BF16, name="wg", tag="wg", bufs=2, align_bytes=64)
+                for gate in range(2):
+                    dst = wg[:, gate].bitcast(F32).rearrange("p g (r u) -> p g r u", u=2)
+                    if gate == 0 and c % 2 == 0:
+                        nc.vector.tensor_copy(out=dst, in_=banks[("fw", c, gate)])
+                    else:
+                        nc.scalar.copy(out=dst, in_=banks[("fw", c, gate)])
                 nc.vector.quantize_mx(
-                    out=w_codes[:, slot, :].bitcast(FP8X4),
-                    scales=w_scales[:, slot, :],
-                    in_=banks[("wg", i)][:].rearrange("p g n -> p (g n)"),
+                    out=w_codes[:, c].rearrange("p a n -> p (a n)").bitcast(FP8X4),
+                    scales=w_scales[:, c].rearrange("p a n -> p (a n)"),
+                    in_=wg[:].rearrange("p a g n -> p (a g n)"),
                 )
 
             def mxp(s):
-                q = s // 8
-                c = s % 8
+                q = s // NC
+                c = s % NC
                 xc, xs = xc_tiles[q]
                 for gate in range(2):
-                    slot = gate * NC + c
                     acc = psum.tile([P, 512], F32, name="acc", tag="mx", bufs=MX_BUFS)
                     for g in range(2):
                         nc.tensor.matmul_mx(
                             out=acc[:],
-                            lhsT=w_codes[:, slot, g * P:(g + 1) * P].bitcast(FP8X4),
-                            lhsT_scale=w_scales[:, slot, g * P:(g + 1) * P],
+                            lhsT=w_codes[:, c, gate, g * P:(g + 1) * P].bitcast(FP8X4),
+                            lhsT_scale=w_scales[:, c, gate, g * P:(g + 1) * P],
                             rhs=xc[:, g, :].bitcast(FP8X4),
                             rhs_scale=xs[:, g, :],
                             start=(g == 0),
@@ -187,14 +176,14 @@ def tile_cell_kernel(tc, xt, ht_minus_1, Wa, Wx, ba, bx, Lambda, out_0, out_1):
                         )
                     banks[("mx", s, gate)] = acc
 
-            def gate_slot(s, square_on_s):
+            def gate_slot(s):
                 n = s // 4
                 cc = s % 4
-                c = s % 8
+                c = s % NC
                 if cc == 0:
                     ta = bl.tile([P, 4, 4, P], F32, name="ta", tag="ta", bufs=2)
                     tx = bl.tile([P, 4, 4, P], F32, name="tx", tag="tx", bufs=2)
-                    a2 = bl.tile([P, 4, 4, P], F32, name="a2", tag="a2", bufs=A2_BUFS)
+                    a2 = bl.tile([P, 4, 4, P], F32, name="a2", tag="a2", bufs=3)
                     units[n] = (ta, tx, a2)
                 ta, tx, a2 = units[n]
                 for gate, dst in ((0, ta), (1, tx)):
@@ -207,10 +196,7 @@ def tile_cell_kernel(tc, xt, ht_minus_1, Wa, Wx, ba, bx, Lambda, out_0, out_1):
                     )
                 nc.scalar.activation(out=ta[:, :, cc, :], in_=ta[:, :, cc, :], func=ACT.Exp,
                                      scale=nhc[:, c:c + 1], bias=nhc[:, c:c + 1])
-                if square_on_s:
-                    nc.scalar.activation(out=a2[:, :, cc, :], in_=ta[:, :, cc, :], func=ACT.Square)
-                else:
-                    nc.gpsimd.tensor_tensor(out=a2[:, :, cc, :], in0=ta[:, :, cc, :], in1=ta[:, :, cc, :], op=ALU.mult)
+                nc.gpsimd.tensor_tensor(out=a2[:, :, cc, :], in0=ta[:, :, cc, :], in1=ta[:, :, cc, :], op=ALU.mult)
 
             def back(src, jj):
                 bk = psum.tile([P, 512], F32, name="bk", tag="tp", bufs=TP_BUFS)
@@ -222,7 +208,7 @@ def tile_cell_kernel(tc, xt, ht_minus_1, Wa, Wx, ba, bx, Lambda, out_0, out_1):
                 f = units[n][2][:].rearrange("p j c r -> p (j c r)")
                 nc.scalar.activation(out=f, in_=f, func=ACT.Sqrt, scale=-0.25, bias=quarter[:, 0:1])
 
-            def do_job(job, on_v):
+            def do_job(job):
                 kind, n, jj = job
                 q = n // 2
                 half = slice((n % 2) * 512, (n % 2) * 512 + 512)
@@ -242,42 +228,40 @@ def tile_cell_kernel(tc, xt, ht_minus_1, Wa, Wx, ba, bx, Lambda, out_0, out_1):
                                                    op0=ALU.add, op1=ALU.mult)
                     banks[("ix", n, jj)] = ix
                     if n % 2 == 1 and jj == 3 and q + 3 < NQ:
-                        load_x(q + 3, False)
+                        load_x(q + 3)
                 else:
                     bk = back(units[n][2], jj)
                     bt = tmp.tile([P, 512], F32, name="bt", tag="bt", bufs=3)
                     nc.vector.tensor_tensor(out=bt[:], in0=bk[:], in1=banks[("ix", n, jj)][:], op=ALU.mult)
-                    if on_v:
-                        nc.vector.tensor_tensor(out=o, in0=o, in1=bt[:], op=ALU.add)
-                    else:
-                        nc.gpsimd.tensor_tensor(out=o, in0=o, in1=bt[:], op=ALU.add)
+                    nc.gpsimd.tensor_tensor(out=o, in0=o, in1=bt[:], op=ALU.add)
                     pending.append((n, jj))
 
-            def reduce_one():
+            def finish_one():
                 n, jj = pending.pop(0)
+                if n % 2 == 0:
+                    return
                 q = n // 2
-                t = 4 * n + jj
-                half = slice((n % 2) * 512, (n % 2) * 512 + 512)
-                if q >= WIDE_RD:
-                    nc.vector.tensor_reduce(out=stats[:, t:t + 1], in_=outs[q][:, jj, half], axis=AX.X, op=ALU.max,
+                j = 4 * q + jj
+                if q == NQ - 1:
+                    nc.vector.tensor_reduce(out=stats[:, j:j + 1], in_=outs[q][:, jj, :], axis=AX.X, op=ALU.max,
                                             apply_absolute_value=True)
-                elif n % 2 == 1:
-                    nc.vector.tensor_reduce(out=stats[:, t:t + 1], in_=outs[q][:, jj, :], axis=AX.X, op=ALU.max,
-                                            apply_absolute_value=True)
-                if n % 2 == 1:
-                    nc.sync.dma_start(out=o0_view[:, 4 * q + jj, :], in_=outs[q][:, jj, :])
+                elif jj % 2 == 1:
+                    nc.vector.tensor_reduce(out=stats[:, j:j + 1],
+                                            in_=outs[q][:, jj - 1:jj + 1, :].rearrange("p j c -> p (j c)"),
+                                            axis=AX.X, op=ALU.max, apply_absolute_value=True)
+                nc.sync.dma_start(out=o0_view[:, j, :], in_=outs[q][:, jj, :])
 
             pending = []
 
-            load_x(0, True)
-            for i in range(W_BUFS):
-                load_w(i)
+            load_x(0)
+            for i in range(2 * NC):
+                load_w(i // 2, i % 2)
                 if i + 1 == H0_AFTER:
                     load_h(0)
                 if i + 1 == X1_AFTER:
-                    load_x(1, False)
+                    load_x(1)
             load_h(1)
-            load_x(2, False)
+            load_x(2)
             vps = psum.tile([P, P], BF16, name="vps", tag="tp", bufs=TP_BUFS)
             nc.tensor.transpose(vps[:], vecs[:], identb[:])
             cols = const.tile([P, 24], F32, name="cols")
@@ -295,16 +279,15 @@ def tile_cell_kernel(tc, xt, ht_minus_1, Wa, Wx, ba, bx, Lambda, out_0, out_1):
             nc.scalar.activation(out=warm[:], in_=zero[:], func=ACT.Tanh)
             for jj in range(4):
                 fx_turn(0, jj)
-                fx_copy(0, jj, False)
+                fx_copy(0, jj)
             fx_quant(0)
             sp = const.tile([P, NC], F32, name="sp")
             nc.vector.scalar_tensor_tensor(out=sp[:], in0=lam, scalar=0.0, in1=sp_l[:], op0=ALU.max, op1=ALU.add)
             nhc = const.tile([P, NC], F32, name="nhc")
             nc.vector.tensor_scalar(out=nhc[:], in0=sp[:], scalar1=-4.0, scalar2=None, op0=ALU.mult)
-            for i in range(4):
-                fw_turn(i)
-                fw_copy(i)
-                fw_quant(i)
+            for c in range(2):
+                fw_turn(c)
+                fw_finish(c)
             mxp(0)
 
             early = []
@@ -312,47 +295,39 @@ def tile_cell_kernel(tc, xt, ht_minus_1, Wa, Wx, ba, bx, Lambda, out_0, out_1):
 
             def emit(queue, k):
                 for r in range(min(k, len(queue))):
-                    do_job(queue.pop(0), False)
+                    do_job(queue.pop(0))
                     if len(pending) > RD_LAG:
-                        reduce_one()
+                        finish_one()
 
-            run_of = {}
-            for run in RUNS:
-                run_of[run[-1]] = run
-
-            for s in range(32):
-                q = s // 8
-                i = s % 8
+            for s in range(NSLOT):
+                q = s // NC
+                i = s % NC
                 n = s // 4
-                window = (s % 4 == 3) and (n in run_of)
-                if i < 7:
+                if i < NC - 1:
                     mxp(s + 1)
-                if q == 0 and s + 2 < 8:
-                    for w in (2 * (s + 2), 2 * (s + 2) + 1):
-                        fw_turn(w)
-                fx_now = FX_AT[q] <= i < FX_AT[q] + 4 and q + 1 < NQ
+                if q == 0 and s + 2 < NC:
+                    fw_turn(s + 2)
+                fx_now = q + 1 < NQ and FX_AT[q] <= i < FX_AT[q] + 4
                 if fx_now:
                     fx_turn(q + 1, i - FX_AT[q])
-                gate_slot(s, window and SQ_LAST_ON_S)
-                if q == 0 and s + 2 < 8:
-                    for w in (2 * (s + 2), 2 * (s + 2) + 1):
-                        fw_copy(w)
-                        fw_quant(w)
+                gate_slot(s)
+                if q == 0 and s + 2 < NC:
+                    fw_finish(s + 2)
                 if fx_now:
-                    fx_copy(q + 1, i - FX_AT[q], (i - FX_AT[q]) in X_ON_S[q])
+                    fx_copy(q + 1, i - FX_AT[q])
                     if i == FX_AT[q] + 3:
                         fx_quant(q + 1)
-                if i == 7 and q + 1 < NQ:
+                if i == NC - 1 and q + 1 < NQ:
                     mxp(s + 1)
                 if s % 4 == 3:
                     for jj in range(4):
                         early.append(("a", n, jj))
                         early.append(("x", n, jj))
-                if window:
-                    for u in run_of[n]:
-                        root(u)
+                if i == NC - 1:
+                    root(n - 1)
+                    root(n)
                     emit(early, EARLY_IN_WINDOW)
-                    for u in run_of[n]:
+                    for u in (n - 1, n):
                         for jj in range(4):
                             late.append(("s", u, jj))
                     emit(late, LATE_IN_WINDOW)
@@ -360,12 +335,9 @@ def tile_cell_kernel(tc, xt, ht_minus_1, Wa, Wx, ba, bx, Lambda, out_0, out_1):
                     emit(late, LATE_PER_SLOT)
                     emit(early, EARLY_PER_SLOT)
             emit(early, len(early))
-            while late:
-                do_job(late.pop(0), len(late) % 8 in TAIL_ON_V)
-                if len(pending) > TAIL_LAG:
-                    reduce_one()
+            emit(late, len(late))
             while pending:
-                reduce_one()
+                finish_one()
 
         pm = const.tile([P, 1], F32, name="pm")
         nc.vector.tensor_reduce(out=pm[:], in_=stats[:], axis=AX.X, op=ALU.max)

@@ -158,11 +158,11 @@ def tile_cell_kernel(tc, xt, ht_minus_1, Wa, Wx, ba, bx, Lambda, out_0, out_1):
                     in_=wg[:].rearrange("p a g n -> p (a g n)"),
                 )
 
-            def mxp(s):
+            def mxp(s, gates=(0, 1)):
                 q = s // NC
                 c = s % NC
                 xc, xs = xc_tiles[q]
-                for gate in range(2):
+                for gate in gates:
                     acc = psum.tile([P, 512], F32, name="acc", tag="mx", bufs=MX_BUFS)
                     for g in range(2):
                         nc.tensor.matmul_mx(
@@ -304,7 +304,7 @@ def tile_cell_kernel(tc, xt, ht_minus_1, Wa, Wx, ba, bx, Lambda, out_0, out_1):
                 i = s % NC
                 n = s // 4
                 if i < NC - 1:
-                    mxp(s + 1)
+                    mxp(s + 1, (0,))
                 if q == 0 and s + 2 < NC:
                     fw_turn(s + 2)
                 fx_now = q + 1 < NQ and FX_AT[q] <= i < FX_AT[q] + 4
@@ -317,8 +317,6 @@ def tile_cell_kernel(tc, xt, ht_minus_1, Wa, Wx, ba, bx, Lambda, out_0, out_1):
                     fx_copy(q + 1, i - FX_AT[q])
                     if i == FX_AT[q] + 3:
                         fx_quant(q + 1)
-                if i == NC - 1 and q + 1 < NQ:
-                    mxp(s + 1)
                 if s % 4 == 3:
                     for jj in range(4):
                         early.append(("a", n, jj))
@@ -326,13 +324,20 @@ def tile_cell_kernel(tc, xt, ht_minus_1, Wa, Wx, ba, bx, Lambda, out_0, out_1):
                 if i == NC - 1:
                     root(n - 1)
                     root(n)
-                    emit(early, EARLY_IN_WINDOW)
+                    emit(early, 3)
+                    if q + 1 < NQ:
+                        mxp(s + 1, (0,))
+                    emit(early, EARLY_IN_WINDOW - 3)
                     for u in (n - 1, n):
                         for jj in range(4):
                             late.append(("s", u, jj))
-                    emit(late, LATE_IN_WINDOW)
+                    emit(late, 1)
+                    if q + 1 < NQ:
+                        mxp(s + 1, (1,))
+                    emit(late, LATE_IN_WINDOW - 1)
                 else:
                     emit(late, LATE_PER_SLOT)
+                    mxp(s + 1, (1,))
                     emit(early, EARLY_PER_SLOT)
             emit(early, len(early))
             emit(late, len(late))

@@ -25,15 +25,25 @@ NSLOT = NQ * NC
 VS = 2752
 MX_BUFS = 4
 TP_BUFS = 4
-IX_BUFS = 10
-FX_AT = (2, 2, 2)
+RUNS = ((0, 1), (2, 3), (4, 5), (6, 7))
+A2_BUFS = 3
+IX_BUFS = 3
+TA_BUFS = 2
+TX_BUFS = 3
+FX_AT = 2
+WL = 2
 LATE_PER_SLOT = 1
-EARLY_PER_SLOT = 2
-EARLY_IN_WINDOW = 6
-LATE_IN_WINDOW = 4
-RD_LAG = 4
-H0_AFTER = 8
+EARLY_PER_SLOT = 1
+EARLY_IN_WINDOW = 4
+LATE_IN_WINDOW = 0
+W_PER_SLOT = 1
+W_IN_WINDOW = 3
+RD_LAG = 1
+H0_AFTER = 6
 X1_AFTER = 12
+W_ON_V = 1
+X_ON_V = 0
+TAIL_W_ON_V = 0
 
 
 def tile_cell_kernel(tc, xt, ht_minus_1, Wa, Wx, ba, bx, Lambda, out_0, out_1):
@@ -42,7 +52,7 @@ def tile_cell_kernel(tc, xt, ht_minus_1, Wa, Wx, ba, bx, Lambda, out_0, out_1):
     h_view = ht_minus_1.rearrange("(p j) k -> p j k", j=NJ)
     o0_view = out_0.rearrange("(p j) c -> p j c", j=NJ)
     o1_view = out_1.rearrange("(p j) c -> p (j c)", j=NJ)
-    w_dram = (Wa, Wx)
+    w_view = (Wa.rearrange("(a m t) k -> a t m k", a=2, t=4), Wx.rearrange("(a m t) k -> a t m k", a=2, t=4))
 
     with ExitStack() as ctx:
         ctx.enter_context(tc.manual_schedule())
@@ -53,19 +63,16 @@ def tile_cell_kernel(tc, xt, ht_minus_1, Wa, Wx, ba, bx, Lambda, out_0, out_1):
 
         w_codes = keep.tile([P, NC, 2, 256], U32, name="w_codes", align_bytes=64)
         w_scales = keep.tile([P, NC, 2, 256], U8, name="w_scales", align_bytes=64)
-        stats = const.tile([P, NJ], F32, name="stats")
+        stats = const.tile([P, 2 * NJ], F32, name="stats")
         nc.vector.memset(stats[:], 0.0)
         outs = []
         for q in range(2):
             o_q = keep.tile([P, 4, D], F32, name="o_q%d" % q)
             outs.append(o_q)
 
-        vecs = const.tile([P, P], BF16, name="vecs")
-        nc.vector.memset(vecs[:], 0.0)
+        vecs = const.tile([P, 3, 4, 4], BF16, name="vecs")
         for i, v in enumerate((ba, bx, Lambda)):
-            nc.scalar.dma_start(out=vecs[8 * i:8 * i + 8, :], in_=v.rearrange("o (c p) -> (o c) p", p=P))
-        identb = const.tile([P, P], BF16, name="identb")
-        make_identity(nc, identb[:])
+            nc.scalar.dma_start(out=vecs[:, i, 0:2, :], in_=v.rearrange("o (a p t) -> p (o a) t", a=2, t=4))
         ident = const.tile([P, P], F32, name="ident")
         make_identity(nc, ident[:])
         zero = const.tile([P, 1], F32, name="zero")
@@ -76,21 +83,25 @@ def tile_cell_kernel(tc, xt, ht_minus_1, Wa, Wx, ba, bx, Lambda, out_0, out_1):
         nc.vector.memset(quarter[:], 0.25)
 
         with ExitStack() as ph1:
-            xraw = ph1.enter_context(tc.tile_pool(name="xraw", bufs=3))
+            xraw = ph1.enter_context(tc.tile_pool(name="xraw", bufs=2))
             hraw = ph1.enter_context(tc.tile_pool(name="hraw", bufs=2))
             grp = ph1.enter_context(tc.tile_pool(name="grp", bufs=1))
             xq = ph1.enter_context(tc.tile_pool(name="xq", bufs=2))
             bl = ph1.enter_context(tc.tile_pool(name="bl", bufs=2))
-            tmp = ph1.enter_context(tc.tile_pool(name="tmp", bufs=4))
 
             x_tiles = {}
             h_tiles = {}
             w_tiles = {}
             xg_tiles = {}
-            wg_tiles = {}
             xc_tiles = {}
-            units = {}
+            ta_tiles = {}
+            a2_tiles = {}
+            ix_tiles = {}
             banks = {}
+            pending = []
+            early = []
+            late = []
+            wq = []
 
             def load_x(q):
                 xr = xraw.tile([P, 4, D], BF16, name="xr", tag="xr")
@@ -108,7 +119,7 @@ def tile_cell_kernel(tc, xt, ht_minus_1, Wa, Wx, ba, bx, Lambda, out_0, out_1):
 
             def load_w(c, gate):
                 wr = share.tile([P, D], BF16, name="wr", tag="wr", bufs=2 * NC, offset=0)
-                nc.sync.dma_start(out=wr[:], in_=w_dram[gate][c * P:(c + 1) * P, :])
+                nc.sync.dma_start(out=wr[:], in_=w_view[gate][c // 4, c % 4])
                 w_tiles[(c, gate)] = wr
 
             def turn(rows_bf16):
@@ -121,16 +132,18 @@ def tile_cell_kernel(tc, xt, ht_minus_1, Wa, Wx, ba, bx, Lambda, out_0, out_1):
 
             def fx_turn(q, jj):
                 if jj == 0:
-                    xg_tiles[q] = grp.tile([P, 2, 2048], BF16, name="xg", tag="xg", bufs=1, align_bytes=64)
+                    xg_tiles[q] = grp.tile([P, 2, 2048], BF16, name="xg", tag="xg", bufs=2, align_bytes=64)
                 banks[("fx", q, jj)] = turn(x_tiles[q][:, jj, :])
 
             def fx_copy(q, jj):
                 xgw = xg_tiles[q][:].bitcast(F32)
                 dst = xgw[:, :, jj * 256:(jj + 1) * 256].rearrange("p g (r u) -> p g r u", u=2)
-                if q == 0:
+                if q == 0 or jj < X_ON_V:
                     nc.vector.tensor_copy(out=dst, in_=banks[("fx", q, jj)])
                 else:
                     nc.scalar.copy(out=dst, in_=banks[("fx", q, jj)])
+                if jj == 3 and q + 2 < NQ:
+                    load_x(q + 2)
 
             def fx_quant(q):
                 xg = xg_tiles[q]
@@ -148,7 +161,7 @@ def tile_cell_kernel(tc, xt, ht_minus_1, Wa, Wx, ba, bx, Lambda, out_0, out_1):
                 wg = grp.tile([P, 2, 2, 512], BF16, name="wg", tag="wg", bufs=2, align_bytes=64)
                 for gate in range(2):
                     dst = wg[:, gate].bitcast(F32).rearrange("p g (r u) -> p g r u", u=2)
-                    if gate == 0 and c % 2 == 0:
+                    if gate < W_ON_V:
                         nc.vector.tensor_copy(out=dst, in_=banks[("fw", c, gate)])
                     else:
                         nc.scalar.copy(out=dst, in_=banks[("fw", c, gate)])
@@ -158,100 +171,109 @@ def tile_cell_kernel(tc, xt, ht_minus_1, Wa, Wx, ba, bx, Lambda, out_0, out_1):
                     in_=wg[:].rearrange("p a g n -> p (a g n)"),
                 )
 
-            def mxp(s, gates=(0, 1)):
+            def mxp(s, gate):
                 q = s // NC
                 c = s % NC
                 xc, xs = xc_tiles[q]
-                for gate in gates:
-                    acc = psum.tile([P, 512], F32, name="acc", tag="mx", bufs=MX_BUFS)
-                    for g in range(2):
-                        nc.tensor.matmul_mx(
-                            out=acc[:],
-                            lhsT=w_codes[:, c, gate, g * P:(g + 1) * P].bitcast(FP8X4),
-                            lhsT_scale=w_scales[:, c, gate, g * P:(g + 1) * P],
-                            rhs=xc[:, g, :].bitcast(FP8X4),
-                            rhs_scale=xs[:, g, :],
-                            start=(g == 0),
-                            stop=(g == 1),
-                        )
-                    banks[("mx", s, gate)] = acc
+                acc = psum.tile([P, 512], F32, name="acc", tag="mx", bufs=MX_BUFS)
+                for g in range(2):
+                    nc.tensor.matmul_mx(
+                        out=acc[:],
+                        lhsT=w_codes[:, c, gate, g * P:(g + 1) * P].bitcast(FP8X4),
+                        lhsT_scale=w_scales[:, c, gate, g * P:(g + 1) * P],
+                        rhs=xc[:, g, :].bitcast(FP8X4),
+                        rhs_scale=xs[:, g, :],
+                        start=(g == 0),
+                        stop=(g == 1),
+                    )
+                banks[("mx", s, gate)] = acc
 
             def gate_slot(s):
+                q = s // NC
                 n = s // 4
-                cc = s % 4
+                t = s % 4
                 c = s % NC
-                if cc == 0:
-                    ta = bl.tile([P, 4, 4, P], F32, name="ta", tag="ta", bufs=2)
-                    tx = bl.tile([P, 4, 4, P], F32, name="tx", tag="tx", bufs=2)
-                    a2 = bl.tile([P, 4, 4, P], F32, name="a2", tag="a2", bufs=3)
-                    units[n] = (ta, tx, a2)
-                ta, tx, a2 = units[n]
-                for gate, dst in ((0, ta), (1, tx)):
-                    nc.scalar.activation(
-                        out=dst[:, :, cc, :],
-                        in_=banks[("mx", s, gate)][:].rearrange("p (j r) -> p j r", j=4),
-                        func=ACT.Tanh,
-                        scale=0.5,
-                        bias=hb[:, gate * NC + c:gate * NC + c + 1],
-                    )
-                nc.scalar.activation(out=ta[:, :, cc, :], in_=ta[:, :, cc, :], func=ACT.Exp,
-                                     scale=nhc[:, c:c + 1], bias=nhc[:, c:c + 1])
-                nc.gpsimd.tensor_tensor(out=a2[:, :, cc, :], in0=ta[:, :, cc, :], in1=ta[:, :, cc, :], op=ALU.mult)
+                if t == 0:
+                    ta_tiles[n] = bl.tile([P, 4, 4, P], F32, name="ta", tag="ta", bufs=TA_BUFS)
+                    a2_tiles[n] = bl.tile([P, 4, 4, P], F32, name="a2", tag="a2", bufs=A2_BUFS)
+                    ix_tiles[n] = bl.tile([P, 4, 4, P], F32, name="ix", tag="ix", bufs=IX_BUFS)
+                ta = ta_tiles[n][:, :, t, :]
+                tx = bl.tile([P, 4, P], F32, name="tx", tag="tx", bufs=TX_BUFS)
+                for gate, dst in ((0, ta), (1, tx[:])):
+                    nc.scalar.activation(out=dst, in_=banks[("mx", s, gate)][:].rearrange("p (j r) -> p j r", j=4),
+                                         func=ACT.Tanh, scale=0.5, bias=hb[:, gate * NC + c:gate * NC + c + 1])
+                nc.vector.scalar_tensor_tensor(out=ix_tiles[n][:, :, t, :], in0=tx[:], scalar=1.0,
+                                               in1=xg_tiles[q][:, c // 4, t:2048:4].rearrange("p (j r) -> p j r", j=4),
+                                               op0=ALU.add, op1=ALU.mult)
+                nc.scalar.activation(out=ta, in_=ta, func=ACT.Exp, scale=nhc[:, c:c + 1], bias=nhc[:, c:c + 1])
+                nc.gpsimd.tensor_tensor(out=a2_tiles[n][:, :, t, :], in0=ta, in1=ta, op=ALU.mult)
 
-            def back(src, jj):
-                bk = psum.tile([P, 512], F32, name="bk", tag="tp", bufs=TP_BUFS)
-                for cc in range(4):
-                    nc.tensor.transpose(bk[:, cc * P:(cc + 1) * P], src[:, jj, cc, :], ident[:])
-                return bk
+            def out_tile(q):
+                if q == len(outs):
+                    o_late = share.tile([P, 4, D], F32, name="o_late%d" % q, offset=(q - 2) * 16384)
+                    outs.append(o_late)
+                return outs[q]
 
-            def root(n):
-                f = units[n][2][:].rearrange("p j c r -> p (j c r)")
-                nc.scalar.activation(out=f, in_=f, func=ACT.Sqrt, scale=-0.25, bias=quarter[:, 0:1])
+            def root(n, parts):
+                f = a2_tiles[n][:].rearrange("p j c r -> p (j c r)")
+                w = 2048 // parts
+                for k in range(parts):
+                    nc.scalar.activation(out=f[:, k * w:(k + 1) * w], in_=f[:, k * w:(k + 1) * w], func=ACT.Sqrt,
+                                         scale=-0.25, bias=quarter[:, 0:1])
+                for jj in range(4):
+                    wq.append((n, jj))
+
+            def emit_w(k, on_vector=0):
+                for r in range(min(k, len(wq))):
+                    n, jj = wq.pop(0)
+                    f = a2_tiles[n][:, jj].rearrange("p c r -> p (c r)")
+                    eng = nc.vector if r < on_vector else nc.gpsimd
+                    eng.tensor_tensor(out=f, in0=f, in1=ix_tiles[n][:, jj].rearrange("p c r -> p (c r)"), op=ALU.mult)
+                    late.append(("s", n, jj))
 
             def do_job(job):
                 kind, n, jj = job
                 q = n // 2
                 half = slice((n % 2) * 512, (n % 2) * 512 + 512)
-                if q == len(outs):
-                    o_late = share.tile([P, 4, D], F32, name="o_late%d" % q, offset=(q - 2) * 16384)
-                    outs.append(o_late)
-                o = outs[q][:, jj, half]
+                bk = psum.tile([P, 4, P], F32, name="bk", tag="tp", bufs=TP_BUFS)
+                src = ta_tiles[n] if kind == "a" else a2_tiles[n]
+                for t in range(4):
+                    nc.tensor.transpose(bk[:, t, :], src[:, jj, t, :], ident[:])
+                o = out_tile(q)[:, jj, half].rearrange("p (m t) -> p m t", t=4)
+                bkv = bk[:].rearrange("p t m -> p m t")
                 if kind == "a":
-                    bk = back(units[n][0], jj)
-                    nc.vector.tensor_tensor(out=o, in0=bk[:], in1=h_tiles[q][:, jj, half], op=ALU.mult)
+                    nc.vector.tensor_tensor(out=o, in0=bkv, in1=h_tiles[q][:, jj, half].rearrange("p (m t) -> p m t", t=4),
+                                            op=ALU.mult)
                     if n % 2 == 1 and jj == 3 and q + 2 < NQ:
                         load_h(q + 2)
-                elif kind == "x":
-                    bk = back(units[n][1], jj)
-                    ix = tmp.tile([P, 512], F32, name="ix", tag="ix", bufs=IX_BUFS)
-                    nc.vector.scalar_tensor_tensor(out=ix[:], in0=bk[:], scalar=1.0, in1=x_tiles[q][:, jj, half],
-                                                   op0=ALU.add, op1=ALU.mult)
-                    banks[("ix", n, jj)] = ix
-                    if n % 2 == 1 and jj == 3 and q + 3 < NQ:
-                        load_x(q + 3)
                 else:
-                    bk = back(units[n][2], jj)
-                    bt = tmp.tile([P, 512], F32, name="bt", tag="bt", bufs=3)
-                    nc.vector.tensor_tensor(out=bt[:], in0=bk[:], in1=banks[("ix", n, jj)][:], op=ALU.mult)
-                    nc.gpsimd.tensor_tensor(out=o, in0=o, in1=bt[:], op=ALU.add)
+                    nc.vector.tensor_tensor(out=o, in0=bkv, in1=o, op=ALU.add)
                     pending.append((n, jj))
 
             def finish_one():
                 n, jj = pending.pop(0)
-                if n % 2 == 0:
-                    return
                 q = n // 2
                 j = 4 * q + jj
                 if q == NQ - 1:
-                    nc.vector.tensor_reduce(out=stats[:, j:j + 1], in_=outs[q][:, jj, :], axis=AX.X, op=ALU.max,
-                                            apply_absolute_value=True)
-                elif jj % 2 == 1:
-                    nc.vector.tensor_reduce(out=stats[:, j:j + 1],
-                                            in_=outs[q][:, jj - 1:jj + 1, :].rearrange("p j c -> p (j c)"),
-                                            axis=AX.X, op=ALU.max, apply_absolute_value=True)
+                    half = slice((n % 2) * 512, (n % 2) * 512 + 512)
+                    nc.vector.tensor_reduce(out=stats[:, 2 * j + n % 2:2 * j + n % 2 + 1], in_=outs[q][:, jj, half], axis=AX.X,
+                                            op=ALU.max, apply_absolute_value=True)
+                    if n % 2 == 0:
+                        return
+                else:
+                    if n % 2 == 0:
+                        return
+                    if jj % 2 == 1:
+                        nc.vector.tensor_reduce(out=stats[:, 2 * j:2 * j + 1],
+                                                in_=outs[q][:, jj - 1:jj + 1, :].rearrange("p j c -> p (j c)"),
+                                                axis=AX.X, op=ALU.max, apply_absolute_value=True)
                 nc.sync.dma_start(out=o0_view[:, j, :], in_=outs[q][:, jj, :])
 
-            pending = []
+            def emit(queue, k):
+                for r in range(min(k, len(queue))):
+                    do_job(queue.pop(0))
+                    if len(pending) > RD_LAG:
+                        finish_one()
 
             load_x(0)
             for i in range(2 * NC):
@@ -261,14 +283,11 @@ def tile_cell_kernel(tc, xt, ht_minus_1, Wa, Wx, ba, bx, Lambda, out_0, out_1):
                 if i + 1 == X1_AFTER:
                     load_x(1)
             load_h(1)
-            load_x(2)
-            vps = psum.tile([P, P], BF16, name="vps", tag="tp", bufs=TP_BUFS)
-            nc.tensor.transpose(vps[:], vecs[:], identb[:])
-            cols = const.tile([P, 24], F32, name="cols")
-            nc.vector.tensor_copy(out=cols[:], in_=vps[:, 0:24])
+            cols24 = const.tile([P, 24], F32, name="cols24")
+            nc.vector.tensor_copy(out=cols24[:].rearrange("p (i a t) -> p i a t", i=3, t=4), in_=vecs[:, :, 0:2, :])
             hb = const.tile([P, 16], F32, name="hb")
-            nc.vector.tensor_scalar(out=hb[:], in0=cols[:, 0:16], scalar1=0.5, scalar2=None, op0=ALU.mult)
-            lam = cols[:, 16:24]
+            nc.vector.tensor_scalar(out=hb[:], in0=cols24[:, 0:16], scalar1=0.5, scalar2=None, op0=ALU.mult)
+            lam = cols24[:, 16:24]
             sp_a = const.tile([P, NC], F32, name="sp_a")
             nc.scalar.activation(out=sp_a[:], in_=lam, func=ACT.Abs)
             sp_e = const.tile([P, NC], F32, name="sp_e")
@@ -285,62 +304,56 @@ def tile_cell_kernel(tc, xt, ht_minus_1, Wa, Wx, ba, bx, Lambda, out_0, out_1):
             nc.vector.scalar_tensor_tensor(out=sp[:], in0=lam, scalar=0.0, in1=sp_l[:], op0=ALU.max, op1=ALU.add)
             nhc = const.tile([P, NC], F32, name="nhc")
             nc.vector.tensor_scalar(out=nhc[:], in0=sp[:], scalar1=-4.0, scalar2=None, op0=ALU.mult)
-            for c in range(2):
+            fw_turn(0)
+            fw_finish(0)
+            for c in range(1, WL):
                 fw_turn(c)
+            mxp(0, 0)
+            mxp(0, 1)
+            for c in range(1, WL):
                 fw_finish(c)
-            mxp(0)
 
-            early = []
-            late = []
-
-            def emit(queue, k):
-                for r in range(min(k, len(queue))):
-                    do_job(queue.pop(0))
-                    if len(pending) > RD_LAG:
-                        finish_one()
+            run_at = {}
+            for units in RUNS:
+                run_at[4 * units[-1] + 3] = units
 
             for s in range(NSLOT):
                 q = s // NC
                 i = s % NC
-                n = s // 4
-                if i < NC - 1:
-                    mxp(s + 1, (0,))
-                if q == 0 and s + 2 < NC:
-                    fw_turn(s + 2)
-                fx_now = q + 1 < NQ and FX_AT[q] <= i < FX_AT[q] + 4
+                more = s + 1 < NSLOT
+                if q == 0 and s + WL < NC:
+                    fw_turn(s + WL)
+                if more:
+                    mxp(s + 1, 0)
+                fx_now = q + 1 < NQ and FX_AT <= i < FX_AT + 4
                 if fx_now:
-                    fx_turn(q + 1, i - FX_AT[q])
+                    fx_turn(q + 1, i - FX_AT)
                 gate_slot(s)
-                if q == 0 and s + 2 < NC:
-                    fw_finish(s + 2)
+                if q == 0 and s + WL < NC:
+                    fw_finish(s + WL)
                 if fx_now:
-                    fx_copy(q + 1, i - FX_AT[q])
-                    if i == FX_AT[q] + 3:
+                    fx_copy(q + 1, i - FX_AT)
+                    if i == FX_AT + 3:
                         fx_quant(q + 1)
+                emit(late, LATE_PER_SLOT)
+                emit_w(W_PER_SLOT)
+                if more:
+                    mxp(s + 1, 1)
+                emit(early, EARLY_PER_SLOT)
                 if s % 4 == 3:
                     for jj in range(4):
-                        early.append(("a", n, jj))
-                        early.append(("x", n, jj))
-                if i == NC - 1:
-                    root(n - 1)
-                    root(n)
-                    emit(early, 3)
-                    if q + 1 < NQ:
-                        mxp(s + 1, (0,))
-                    emit(early, EARLY_IN_WINDOW - 3)
-                    for u in (n - 1, n):
-                        for jj in range(4):
-                            late.append(("s", u, jj))
-                    emit(late, 1)
-                    if q + 1 < NQ:
-                        mxp(s + 1, (1,))
-                    emit(late, LATE_IN_WINDOW - 1)
-                else:
-                    emit(late, LATE_PER_SLOT)
-                    mxp(s + 1, (1,))
-                    emit(early, EARLY_PER_SLOT)
+                        early.append(("a", s // 4, jj))
+                if s in run_at:
+                    units = run_at[s]
+                    for u in units:
+                        root(u, 4 if not more else 1)
+                    emit(early, EARLY_IN_WINDOW)
+                    if more:
+                        emit_w(W_IN_WINDOW)
             emit(early, len(early))
-            emit(late, len(late))
+            while wq or late:
+                emit_w(2, TAIL_W_ON_V)
+                emit(late, 2)
             while pending:
                 finish_one()
 

@@ -23,6 +23,7 @@ NQ = 4
 NC = D // P
 NSLOT = NQ * NC
 VS = 2752
+PIECE = 2048
 MX_BUFS = 4
 TP_BUFS = 4
 RUNS = ((0, 1), (2, 3), (4, 5), (6, 7))
@@ -31,7 +32,8 @@ IX_BUFS = 3
 TA_BUFS = 2
 TX_BUFS = 3
 FX_AT = 2
-WL = 2
+WL = 3
+NWARM = 6
 LATE_PER_SLOT = 1
 EARLY_PER_SLOT = 1
 EARLY_IN_WINDOW = 4
@@ -39,7 +41,7 @@ LATE_IN_WINDOW = 0
 W_PER_SLOT = 1
 W_IN_WINDOW = 3
 RD_LAG = 1
-H0_AFTER = 6
+H0_AFTER = 8
 X1_AFTER = 12
 W_ON_V = 1
 X_ON_V = 0
@@ -70,6 +72,11 @@ def tile_cell_kernel(tc, xt, ht_minus_1, Wa, Wx, ba, bx, Lambda, out_0, out_1):
             o_q = keep.tile([P, 4, D], F32, name="o_q%d" % q)
             outs.append(o_q)
 
+        wz = const.tile([P, 512], BF16, name="wz")
+        nc.vector.memset(wz[:], 0.0)
+        for i in range(NWARM):
+            wp = psum.tile([P, 512], F32, name="wp", tag="mx", bufs=MX_BUFS)
+            nc.tensor.matmul(out=wp[:], lhsT=wz[:, 0:P], rhs=wz[:], start=True, stop=True)
         vecs = const.tile([P, 3, 4, 4], BF16, name="vecs")
         for i, v in enumerate((ba, bx, Lambda)):
             nc.scalar.dma_start(out=vecs[:, i, 0:2, :], in_=v.rearrange("o (a p t) -> p (o a) t", a=2, t=4))
@@ -370,11 +377,14 @@ def tile_cell_kernel(tc, xt, ht_minus_1, Wa, Wx, ba, bx, Lambda, out_0, out_1):
 
         p2 = ctx.enter_context(tc.tile_pool(name="p2", bufs=4))
         for q in range(NQ):
-            lo = q * 4096
             flat = outs[q][:].rearrange("p j c -> p (j c)")
             o8 = p2.tile([P, 4096], FP8, name="o8", tag="o8", bufs=4)
-            nc.vector.tensor_scalar(out=o8[:, 0:VS], in0=flat[:, 0:VS], scalar1=fac[:, 0:1], scalar2=None,
-                                    op0=ALU.mult, saturate=False)
-            nc.scalar.activation(out=o8[:, VS:4096], in_=flat[:, VS:4096], func=ACT.Identity,
-                                 scale=fac[:, 0:1], bias=zero[:, 0:1], saturate=False)
-            nc.sync.dma_start(out=o1_view[:, lo:lo + 4096], in_=o8[:].bitcast(U8))
+            for k in range(4096 // PIECE):
+                a = k * PIECE
+                m = a + (PIECE * VS) // 4096
+                b = a + PIECE
+                nc.vector.tensor_scalar(out=o8[:, a:m], in0=flat[:, a:m], scalar1=fac[:, 0:1], scalar2=None,
+                                        op0=ALU.mult, saturate=False)
+                nc.scalar.activation(out=o8[:, m:b], in_=flat[:, m:b], func=ACT.Identity,
+                                     scale=fac[:, 0:1], bias=zero[:, 0:1], saturate=False)
+                nc.sync.dma_start(out=o1_view[:, q * 4096 + a:q * 4096 + b], in_=o8[:, a:b].bitcast(U8))

@@ -39,7 +39,10 @@ EARLY_PER_SLOT = 1
 EARLY_IN_WINDOW = 4
 LATE_IN_WINDOW = 0
 W_PER_SLOT = 1
-W_IN_WINDOW = 3
+W_IN_WINDOW = 4
+IX_LAG = 0
+SQ_LAG = 1
+SQ_ON_S_FROM = 28
 RD_LAG = 1
 H0_AFTER = 8
 X1_AFTER = 12
@@ -102,6 +105,7 @@ def tile_cell_kernel(tc, xt, ht_minus_1, Wa, Wx, ba, bx, Lambda, out_0, out_1):
             xg_tiles = {}
             xc_tiles = {}
             ta_tiles = {}
+            tx_tiles = {}
             a2_tiles = {}
             ix_tiles = {}
             banks = {}
@@ -206,14 +210,27 @@ def tile_cell_kernel(tc, xt, ht_minus_1, Wa, Wx, ba, bx, Lambda, out_0, out_1):
                     ix_tiles[n] = bl.tile([P, 4, 4, P], F32, name="ix", tag="ix", bufs=IX_BUFS)
                 ta = ta_tiles[n][:, :, t, :]
                 tx = bl.tile([P, 4, P], F32, name="tx", tag="tx", bufs=TX_BUFS)
+                tx_tiles[s] = tx
                 for gate, dst in ((0, ta), (1, tx[:])):
                     nc.scalar.activation(out=dst, in_=banks[("mx", s, gate)][:].rearrange("p (j r) -> p j r", j=4),
                                          func=ACT.Tanh, scale=0.5, bias=hb[:, gate * NC + c:gate * NC + c + 1])
-                nc.vector.scalar_tensor_tensor(out=ix_tiles[n][:, :, t, :], in0=tx[:], scalar=1.0,
+                nc.scalar.activation(out=ta, in_=ta, func=ACT.Exp, scale=nhc[:, c:c + 1], bias=nhc[:, c:c + 1])
+
+            def gated_x(s):
+                q = s // NC
+                n = s // 4
+                t = s % 4
+                c = s % NC
+                nc.vector.scalar_tensor_tensor(out=ix_tiles[n][:, :, t, :], in0=tx_tiles[s][:], scalar=1.0,
                                                in1=xg_tiles[q][:, c // 4, t:2048:4].rearrange("p (j r) -> p j r", j=4),
                                                op0=ALU.add, op1=ALU.mult)
-                nc.scalar.activation(out=ta, in_=ta, func=ACT.Exp, scale=nhc[:, c:c + 1], bias=nhc[:, c:c + 1])
-                nc.gpsimd.tensor_tensor(out=a2_tiles[n][:, :, t, :], in0=ta, in1=ta, op=ALU.mult)
+
+            def square(s):
+                ta = ta_tiles[s // 4][:, :, s % 4, :]
+                if s >= SQ_ON_S_FROM:
+                    nc.scalar.activation(out=a2_tiles[s // 4][:, :, s % 4, :], in_=ta, func=ACT.Square)
+                else:
+                    nc.gpsimd.tensor_tensor(out=a2_tiles[s // 4][:, :, s % 4, :], in0=ta, in1=ta, op=ALU.mult)
 
             def out_tile(q):
                 if q == len(outs):
@@ -335,7 +352,15 @@ def tile_cell_kernel(tc, xt, ht_minus_1, Wa, Wx, ba, bx, Lambda, out_0, out_1):
                 fx_now = q + 1 < NQ and FX_AT <= i < FX_AT + 4
                 if fx_now:
                     fx_turn(q + 1, i - FX_AT)
+                if IX_LAG and s > 0:
+                    gated_x(s - 1)
+                if SQ_LAG and s > 0 and (s - 1) not in run_at and s - 1 < SQ_ON_S_FROM:
+                    square(s - 1)
                 gate_slot(s)
+                if not IX_LAG:
+                    gated_x(s)
+                if not SQ_LAG or s in run_at or s >= SQ_ON_S_FROM:
+                    square(s)
                 if q == 0 and s + WL < NC:
                     fw_finish(s + WL)
                 if fx_now:
@@ -352,6 +377,8 @@ def tile_cell_kernel(tc, xt, ht_minus_1, Wa, Wx, ba, bx, Lambda, out_0, out_1):
                         early.append(("a", s // 4, jj))
                 if s in run_at:
                     units = run_at[s]
+                    if IX_LAG and not more:
+                        gated_x(s)
                     for u in units:
                         root(u, 4 if not more else 1)
                     emit(early, EARLY_IN_WINDOW)

@@ -24,7 +24,8 @@ NC = D // P
 NSLOT = NQ * NC
 VS = 2752
 PIECE = 2048
-MX_BUFS = 4
+MX_BUFS = 3
+XT_BUFS = 1
 TP_BUFS = 4
 RUNS = ((0, 1), (2, 3), (4, 5), (6, 7))
 A2_BUFS = 3
@@ -40,7 +41,7 @@ EARLY_IN_WINDOW = 4
 LATE_IN_WINDOW = 0
 W_PER_SLOT = 1
 W_IN_WINDOW = 4
-IX_LAG = 0
+IX_LAG = 1
 SQ_LAG = 1
 SQ_ON_S_FROM = 28
 RD_LAG = 1
@@ -57,7 +58,7 @@ def tile_cell_kernel(tc, xt, ht_minus_1, Wa, Wx, ba, bx, Lambda, out_0, out_1):
     h_view = ht_minus_1.rearrange("(p j) k -> p j k", j=NJ)
     o0_view = out_0.rearrange("(p j) c -> p j c", j=NJ)
     o1_view = out_1.rearrange("(p j) c -> p (j c)", j=NJ)
-    w_view = (Wa.rearrange("(a m t) k -> a t m k", a=2, t=4), Wx.rearrange("(a m t) k -> a t m k", a=2, t=4))
+    w_view = (Wa.rearrange("(b m e) k -> b e m k", b=4, e=2), Wx.rearrange("(b m e) k -> b e m k", b=4, e=2))
 
     with ExitStack() as ctx:
         ctx.enter_context(tc.manual_schedule())
@@ -80,9 +81,9 @@ def tile_cell_kernel(tc, xt, ht_minus_1, Wa, Wx, ba, bx, Lambda, out_0, out_1):
         for i in range(NWARM):
             wp = psum.tile([P, 512], F32, name="wp", tag="mx", bufs=MX_BUFS)
             nc.tensor.matmul(out=wp[:], lhsT=wz[:, 0:P], rhs=wz[:], start=True, stop=True)
-        vecs = const.tile([P, 3, 4, 4], BF16, name="vecs")
+        vecs = const.tile([P, 3, 8, 2], BF16, name="vecs")
         for i, v in enumerate((ba, bx, Lambda)):
-            nc.scalar.dma_start(out=vecs[:, i, 0:2, :], in_=v.rearrange("o (a p t) -> p (o a) t", a=2, t=4))
+            nc.scalar.dma_start(out=vecs[:, i, 0:4, :], in_=v.rearrange("o (b p e) -> p (o b) e", b=4, e=2))
         ident = const.tile([P, P], F32, name="ident")
         make_identity(nc, ident[:])
         zero = const.tile([P, 1], F32, name="zero")
@@ -93,7 +94,7 @@ def tile_cell_kernel(tc, xt, ht_minus_1, Wa, Wx, ba, bx, Lambda, out_0, out_1):
         nc.vector.memset(quarter[:], 0.25)
 
         with ExitStack() as ph1:
-            xraw = ph1.enter_context(tc.tile_pool(name="xraw", bufs=2))
+            xraw = ph1.enter_context(tc.tile_pool(name="xraw", bufs=3))
             hraw = ph1.enter_context(tc.tile_pool(name="hraw", bufs=2))
             grp = ph1.enter_context(tc.tile_pool(name="grp", bufs=1))
             xq = ph1.enter_context(tc.tile_pool(name="xq", bufs=2))
@@ -103,6 +104,7 @@ def tile_cell_kernel(tc, xt, ht_minus_1, Wa, Wx, ba, bx, Lambda, out_0, out_1):
             h_tiles = {}
             w_tiles = {}
             xg_tiles = {}
+            xt_tiles = {}
             xc_tiles = {}
             ta_tiles = {}
             tx_tiles = {}
@@ -130,7 +132,7 @@ def tile_cell_kernel(tc, xt, ht_minus_1, Wa, Wx, ba, bx, Lambda, out_0, out_1):
 
             def load_w(c, gate):
                 wr = share.tile([P, D], BF16, name="wr", tag="wr", bufs=2 * NC, offset=0)
-                nc.sync.dma_start(out=wr[:], in_=w_view[gate][c // 4, c % 4])
+                nc.sync.dma_start(out=wr[:], in_=w_view[gate][c // 2, c % 2])
                 w_tiles[(c, gate)] = wr
 
             def turn(rows_bf16):
@@ -153,8 +155,18 @@ def tile_cell_kernel(tc, xt, ht_minus_1, Wa, Wx, ba, bx, Lambda, out_0, out_1):
                     nc.vector.tensor_copy(out=dst, in_=banks[("fx", q, jj)])
                 else:
                     nc.scalar.copy(out=dst, in_=banks[("fx", q, jj)])
-                if jj == 3 and q + 2 < NQ:
-                    load_x(q + 2)
+
+            def xt_turn(s):
+                q = s // NC
+                c = s % NC
+                b = c // 2
+                xt = psum.tile([P, 4, P], F32, name="xt", tag="xt", bufs=XT_BUFS)
+                for jj in range(4):
+                    words = x_tiles[q][:, jj, :].bitcast(F32)
+                    nc.tensor.transpose(xt[:, jj, :], words[:, P * b:P * (b + 1)], ident[:])
+                xt_tiles[s // 2] = xt
+                if c == NC - 2 and q + 3 < NQ:
+                    load_x(q + 3)
 
             def fx_quant(q):
                 xg = xg_tiles[q]
@@ -222,7 +234,7 @@ def tile_cell_kernel(tc, xt, ht_minus_1, Wa, Wx, ba, bx, Lambda, out_0, out_1):
                 t = s % 4
                 c = s % NC
                 nc.vector.scalar_tensor_tensor(out=ix_tiles[n][:, :, t, :], in0=tx_tiles[s][:], scalar=1.0,
-                                               in1=xg_tiles[q][:, c // 4, t:2048:4].rearrange("p (j r) -> p j r", j=4),
+                                               in1=xt_tiles[s // 2][:].bitcast(BF16)[:, :, t % 2:256:2],
                                                op0=ALU.add, op1=ALU.mult)
 
             def square(s):
@@ -263,10 +275,10 @@ def tile_cell_kernel(tc, xt, ht_minus_1, Wa, Wx, ba, bx, Lambda, out_0, out_1):
                 src = ta_tiles[n] if kind == "a" else a2_tiles[n]
                 for t in range(4):
                     nc.tensor.transpose(bk[:, t, :], src[:, jj, t, :], ident[:])
-                o = out_tile(q)[:, jj, half].rearrange("p (m t) -> p m t", t=4)
-                bkv = bk[:].rearrange("p t m -> p m t")
+                o = out_tile(q)[:, jj, half].rearrange("p (b m e) -> p b m e", b=2, e=2)
+                bkv = bk[:].rearrange("p (b e) m -> p b m e", e=2)
                 if kind == "a":
-                    nc.vector.tensor_tensor(out=o, in0=bkv, in1=h_tiles[q][:, jj, half].rearrange("p (m t) -> p m t", t=4),
+                    nc.vector.tensor_tensor(out=o, in0=bkv, in1=h_tiles[q][:, jj, half].rearrange("p (b m e) -> p b m e", b=2, e=2),
                                             op=ALU.mult)
                     if n % 2 == 1 and jj == 3 and q + 2 < NQ:
                         load_h(q + 2)
@@ -307,8 +319,9 @@ def tile_cell_kernel(tc, xt, ht_minus_1, Wa, Wx, ba, bx, Lambda, out_0, out_1):
                 if i + 1 == X1_AFTER:
                     load_x(1)
             load_h(1)
+            load_x(2)
             cols24 = const.tile([P, 24], F32, name="cols24")
-            nc.vector.tensor_copy(out=cols24[:].rearrange("p (i a t) -> p i a t", i=3, t=4), in_=vecs[:, :, 0:2, :])
+            nc.vector.tensor_copy(out=cols24[:].rearrange("p (i b e) -> p i b e", i=3, e=2), in_=vecs[:, :, 0:4, :])
             hb = const.tile([P, 16], F32, name="hb")
             nc.vector.tensor_scalar(out=hb[:], in0=cols24[:, 0:16], scalar1=0.5, scalar2=None, op0=ALU.mult)
             lam = cols24[:, 16:24]
@@ -371,6 +384,8 @@ def tile_cell_kernel(tc, xt, ht_minus_1, Wa, Wx, ba, bx, Lambda, out_0, out_1):
                 emit_w(W_PER_SLOT)
                 if more:
                     mxp(s + 1, 1)
+                if s % 2 == 0:
+                    xt_turn(s)
                 emit(early, EARLY_PER_SLOT)
                 if s % 4 == 3:
                     for jj in range(4):

@@ -48,7 +48,7 @@ RD_LAG = 1
 H0_AFTER = 8
 X1_AFTER = 12
 W_ON_V = 1
-X_ON_V = 0
+X_ON_V = 4
 TAIL_W_ON_V = 0
 
 

@@ -24,9 +24,9 @@ NC = D // P
 NSLOT = NQ * NC
 VS = 2752
 PIECE = 2048
-MX_BUFS = 3
+MX_BUFS = 4
 XT_BUFS = 1
-TP_BUFS = 4
+TP_BUFS = 3
 RUNS = ((0, 1), (2, 3), (4, 5), (6, 7))
 A2_BUFS = 3
 IX_BUFS = 3
@@ -36,8 +36,8 @@ FX_AT = 2
 WL = 3
 NWARM = 6
 LATE_PER_SLOT = 1
-EARLY_PER_SLOT = 1
-EARLY_IN_WINDOW = 4
+EARLY_PER_SLOT = 0
+EARLY_IN_WINDOW = 8
 LATE_IN_WINDOW = 0
 W_PER_SLOT = 1
 W_IN_WINDOW = 4
@@ -50,6 +50,10 @@ X1_AFTER = 12
 W_ON_V = 1
 X_ON_V = 4
 TAIL_W_ON_V = 0
+MX_MODE = 2
+ROOT_PARTS = 1
+FX_WINDOW = 0
+LATE_IN_WIN = 0
 
 
 def tile_cell_kernel(tc, xt, ht_minus_1, Wa, Wx, ba, bx, Lambda, out_0, out_1):
@@ -360,9 +364,11 @@ def tile_cell_kernel(tc, xt, ht_minus_1, Wa, Wx, ba, bx, Lambda, out_0, out_1):
                 more = s + 1 < NSLOT
                 if q == 0 and s + WL < NC:
                     fw_turn(s + WL)
-                if more:
+                if more and MX_MODE != 2:
                     mxp(s + 1, 0)
-                fx_now = q + 1 < NQ and FX_AT <= i < FX_AT + 4
+                if more and MX_MODE == 1:
+                    mxp(s + 1, 1)
+                fx_now = q + 1 < NQ and FX_AT <= i < FX_AT + 4 and (q == 0 or not FX_WINDOW)
                 if fx_now:
                     fx_turn(q + 1, i - FX_AT)
                 if IX_LAG and s > 0:
@@ -382,7 +388,9 @@ def tile_cell_kernel(tc, xt, ht_minus_1, Wa, Wx, ba, bx, Lambda, out_0, out_1):
                         fx_quant(q + 1)
                 emit(late, LATE_PER_SLOT)
                 emit_w(W_PER_SLOT)
-                if more:
+                if more and MX_MODE == 2:
+                    mxp(s + 1, 0)
+                if more and MX_MODE != 1:
                     mxp(s + 1, 1)
                 if s % 2 == 0:
                     xt_turn(s)
@@ -395,10 +403,19 @@ def tile_cell_kernel(tc, xt, ht_minus_1, Wa, Wx, ba, bx, Lambda, out_0, out_1):
                     if IX_LAG and not more:
                         gated_x(s)
                     for u in units:
-                        root(u, 4 if not more else 1)
-                    emit(early, EARLY_IN_WINDOW)
+                        root(u, 4 if not more else ROOT_PARTS)
+                    fx_win = FX_WINDOW and q + 2 < NQ
+                    if fx_win:
+                        for jj in range(4):
+                            fx_turn(q + 2, jj)
+                            emit(early, EARLY_IN_WINDOW // 4)
+                            fx_copy(q + 2, jj)
+                        fx_quant(q + 2)
+                    else:
+                        emit(early, EARLY_IN_WINDOW)
                     if more:
                         emit_w(W_IN_WINDOW)
+                        emit(late, LATE_IN_WIN)
             emit(early, len(early))
             while wq or late:
                 emit_w(2, TAIL_W_ON_V)

@@ -44,6 +44,7 @@ W_IN_WINDOW = 4
 IX_LAG = 1
 SQ_LAG = 1
 SQ_ON_S_FROM = 28
+SQ_S_SLOTS = (3, 7)
 RD_LAG = 1
 H0_AFTER = 8
 X1_AFTER = 12
@@ -241,9 +242,12 @@ def tile_cell_kernel(tc, xt, ht_minus_1, Wa, Wx, ba, bx, Lambda, out_0, out_1):
                                                in1=xt_tiles[s // 2][:].bitcast(BF16)[:, :, t % 2:256:2],
                                                op0=ALU.add, op1=ALU.mult)
 
+            def sq_on_s(s):
+                return s >= SQ_ON_S_FROM or (s % NC) in SQ_S_SLOTS
+
             def square(s):
                 ta = ta_tiles[s // 4][:, :, s % 4, :]
-                if s >= SQ_ON_S_FROM:
+                if sq_on_s(s):
                     nc.scalar.activation(out=a2_tiles[s // 4][:, :, s % 4, :], in_=ta, func=ACT.Square)
                 else:
                     nc.gpsimd.tensor_tensor(out=a2_tiles[s // 4][:, :, s % 4, :], in0=ta, in1=ta, op=ALU.mult)
@@ -373,12 +377,12 @@ def tile_cell_kernel(tc, xt, ht_minus_1, Wa, Wx, ba, bx, Lambda, out_0, out_1):
                     fx_turn(q + 1, i - FX_AT)
                 if IX_LAG and s > 0:
                     gated_x(s - 1)
-                if SQ_LAG and s > 0 and (s - 1) not in run_at and s - 1 < SQ_ON_S_FROM:
+                if SQ_LAG and s > 0 and (s - 1) not in run_at and not sq_on_s(s - 1):
                     square(s - 1)
                 gate_slot(s)
                 if not IX_LAG:
                     gated_x(s)
-                if not SQ_LAG or s in run_at or s >= SQ_ON_S_FROM:
+                if not SQ_LAG or s in run_at or sq_on_s(s):
                     square(s)
                 if q == 0 and s + WL < NC:
                     fw_finish(s + WL)

@@ -45,12 +45,21 @@ IX_LAG = 1
 SQ_LAG = 1
 SQ_ON_S_FROM = 28
 SQ_S_SLOTS = (3, 7)
+LAST_SUM = 1
+S_SQ_LAG = 1
+HEAD_TBL = 1
+W0_ON_S = 0
+MX0_FIRST = 0
+Q_APART = 1
+TAIL_RD_LAG = 3
+TAIL_G = (0, 2, 4)
+TAIL_STEP = 2
 RD_LAG = 1
 H0_AFTER = 8
 X1_AFTER = 12
 W_ON_V = 1
 X_ON_V = 4
-TAIL_W_ON_V = 0
+TAIL_W_ON_V = 1
 MX_MODE = 2
 ROOT_PARTS = 1
 FX_WINDOW = 0
@@ -95,6 +104,9 @@ def tile_cell_kernel(tc, xt, ht_minus_1, Wa, Wx, ba, bx, Lambda, out_0, out_1):
         nc.vector.memset(zero[:], 0.0)
         one = const.tile([P, 1], F32, name="one")
         nc.vector.memset(one[:], 1.0)
+        warm = const.tile([P, 1], F32, name="warm")
+        if HEAD_TBL:
+            nc.scalar.activation(out=warm[:], in_=zero[:], func=ACT.Exp)
         quarter = const.tile([P, 1], F32, name="quarter")
         nc.vector.memset(quarter[:], 0.25)
 
@@ -173,6 +185,17 @@ def tile_cell_kernel(tc, xt, ht_minus_1, Wa, Wx, ba, bx, Lambda, out_0, out_1):
                 if c == NC - 2 and q + 3 < NQ:
                     load_x(q + 3)
 
+            def ht_turn(s):
+                q = s // NC
+                b = (s % NC) // 2
+                ht = psum.tile([P, 4, P], F32, name="ht", tag="tp", bufs=TP_BUFS)
+                for jj in range(4):
+                    words = h_tiles[q][:, jj, :].bitcast(F32)
+                    nc.tensor.transpose(ht[:, jj, :], words[:, P * b:P * (b + 1)], ident[:])
+                for s2 in (s, s + 1):
+                    ta = ta_tiles[s2 // 4][:, :, s2 % 4, :]
+                    nc.vector.tensor_tensor(out=ta, in0=ta, in1=ht[:].bitcast(BF16)[:, :, s2 % 2:256:2], op=ALU.mult)
+
             def fx_quant(q):
                 xg = xg_tiles[q]
                 xc = xq.tile([P, 2, 512], U32, name="xc", tag="xc", bufs=2, align_bytes=64)
@@ -189,7 +212,7 @@ def tile_cell_kernel(tc, xt, ht_minus_1, Wa, Wx, ba, bx, Lambda, out_0, out_1):
                 wg = grp.tile([P, 2, 2, 512], BF16, name="wg", tag="wg", bufs=2, align_bytes=64)
                 for gate in range(2):
                     dst = wg[:, gate].bitcast(F32).rearrange("p g (r u) -> p g r u", u=2)
-                    if gate < W_ON_V:
+                    if gate < W_ON_V and not (W0_ON_S and c == 0):
                         nc.vector.tensor_copy(out=dst, in_=banks[("fw", c, gate)])
                     else:
                         nc.scalar.copy(out=dst, in_=banks[("fw", c, gate)])
@@ -231,6 +254,8 @@ def tile_cell_kernel(tc, xt, ht_minus_1, Wa, Wx, ba, bx, Lambda, out_0, out_1):
                 for gate, dst in ((0, ta), (1, tx[:])):
                     nc.scalar.activation(out=dst, in_=banks[("mx", s, gate)][:].rearrange("p (j r) -> p j r", j=4),
                                          func=ACT.Tanh, scale=0.5, bias=hb[:, gate * NC + c:gate * NC + c + 1])
+                    if S_SQ_LAG and gate == 0 and s > 0 and sq_on_s(s - 1) and (s - 1) not in run_at:
+                        square(s - 1)
                 nc.scalar.activation(out=ta, in_=ta, func=ACT.Exp, scale=nhc[:, c:c + 1], bias=nhc[:, c:c + 1])
 
             def gated_x(s):
@@ -281,10 +306,20 @@ def tile_cell_kernel(tc, xt, ht_minus_1, Wa, Wx, ba, bx, Lambda, out_0, out_1):
                 half = slice((n % 2) * 512, (n % 2) * 512 + 512)
                 bk = psum.tile([P, 4, P], F32, name="bk", tag="tp", bufs=TP_BUFS)
                 src = ta_tiles[n] if kind == "a" else a2_tiles[n]
-                for t in range(4):
-                    nc.tensor.transpose(bk[:, t, :], src[:, jj, t, :], ident[:])
                 o = out_tile(q)[:, jj, half].rearrange("p (b m e) -> p b m e", b=2, e=2)
                 bkv = bk[:].rearrange("p (b e) m -> p b m e", e=2)
+                if LAST_SUM and q == NQ - 1:
+                    for t in range(4):
+                        nc.tensor.matmul(out=bk[:, t, :], lhsT=ta_tiles[n][:, jj, t, :], rhs=ident[:], is_transpose=True,
+                                         start=(t == 0), stop=False)
+                    for t in range(4):
+                        nc.tensor.matmul(out=bk[:, t, :], lhsT=a2_tiles[n][:, jj, t, :], rhs=ident[:], is_transpose=True,
+                                         start=False, stop=(t == 3))
+                    nc.scalar.copy(out=o, in_=bkv)
+                    pending.append((n, jj))
+                    return
+                for t in range(4):
+                    nc.tensor.transpose(bk[:, t, :], src[:, jj, t, :], ident[:])
                 if kind == "a":
                     nc.vector.tensor_tensor(out=o, in0=bkv, in1=h_tiles[q][:, jj, half].rearrange("p (b m e) -> p b m e", b=2, e=2),
                                             op=ALU.mult)
@@ -313,10 +348,10 @@ def tile_cell_kernel(tc, xt, ht_minus_1, Wa, Wx, ba, bx, Lambda, out_0, out_1):
                                                 axis=AX.X, op=ALU.max, apply_absolute_value=True)
                 nc.sync.dma_start(out=o0_view[:, j, :], in_=outs[q][:, jj, :])
 
-            def emit(queue, k):
+            def emit(queue, k, lag=RD_LAG):
                 for r in range(min(k, len(queue))):
                     do_job(queue.pop(0))
-                    if len(pending) > RD_LAG:
+                    if len(pending) > lag:
                         finish_one()
 
             load_x(0)
@@ -339,7 +374,6 @@ def tile_cell_kernel(tc, xt, ht_minus_1, Wa, Wx, ba, bx, Lambda, out_0, out_1):
             nc.scalar.activation(out=sp_e[:], in_=sp_a[:], func=ACT.Exp, scale=-1.0)
             sp_l = const.tile([P, NC], F32, name="sp_l")
             nc.scalar.activation(out=sp_l[:], in_=sp_e[:], func=ACT.Ln, bias=one[:, 0:1])
-            warm = const.tile([P, 1], F32, name="warm")
             nc.scalar.activation(out=warm[:], in_=zero[:], func=ACT.Tanh)
             for jj in range(4):
                 fx_turn(0, jj)
@@ -351,10 +385,14 @@ def tile_cell_kernel(tc, xt, ht_minus_1, Wa, Wx, ba, bx, Lambda, out_0, out_1):
             nc.vector.tensor_scalar(out=nhc[:], in0=sp[:], scalar1=-4.0, scalar2=None, op0=ALU.mult)
             fw_turn(0)
             fw_finish(0)
+            if MX0_FIRST:
+                mxp(0, 0)
+                mxp(0, 1)
             for c in range(1, WL):
                 fw_turn(c)
-            mxp(0, 0)
-            mxp(0, 1)
+            if not MX0_FIRST:
+                mxp(0, 0)
+                mxp(0, 1)
             for c in range(1, WL):
                 fw_finish(c)
 
@@ -382,15 +420,19 @@ def tile_cell_kernel(tc, xt, ht_minus_1, Wa, Wx, ba, bx, Lambda, out_0, out_1):
                 gate_slot(s)
                 if not IX_LAG:
                     gated_x(s)
-                if not SQ_LAG or s in run_at or sq_on_s(s):
+                if s in run_at and S_SQ_LAG and sq_on_s(s):
+                    nc.scalar.activation(out=warm[:], in_=one[:], func=ACT.Sqrt)
+                if not SQ_LAG or s in run_at or (sq_on_s(s) and not S_SQ_LAG):
                     square(s)
                 if q == 0 and s + WL < NC:
                     fw_finish(s + WL)
                 if fx_now:
                     fx_copy(q + 1, i - FX_AT)
-                    if i == FX_AT + 3:
+                    if i == FX_AT + 3 and not Q_APART:
                         fx_quant(q + 1)
                 emit(late, LATE_PER_SLOT)
+                if fx_now and i == FX_AT + 3 and Q_APART:
+                    fx_quant(q + 1)
                 emit_w(W_PER_SLOT)
                 if more and MX_MODE == 2:
                     mxp(s + 1, 0)
@@ -399,7 +441,10 @@ def tile_cell_kernel(tc, xt, ht_minus_1, Wa, Wx, ba, bx, Lambda, out_0, out_1):
                 if s % 2 == 0:
                     xt_turn(s)
                 emit(early, EARLY_PER_SLOT)
-                if s % 4 == 3:
+                if LAST_SUM and q == NQ - 1:
+                    if i % 2 == 0 and i > 0:
+                        ht_turn(s - 2)
+                elif s % 4 == 3:
                     for jj in range(4):
                         early.append(("a", s // 4, jj))
                 if s in run_at:
@@ -408,6 +453,8 @@ def tile_cell_kernel(tc, xt, ht_minus_1, Wa, Wx, ba, bx, Lambda, out_0, out_1):
                         gated_x(s)
                     for u in units:
                         root(u, 4 if not more else ROOT_PARTS)
+                    if LAST_SUM and not more:
+                        ht_turn(s - 1)
                     fx_win = FX_WINDOW and q + 2 < NQ
                     if fx_win:
                         for jj in range(4):
@@ -421,9 +468,12 @@ def tile_cell_kernel(tc, xt, ht_minus_1, Wa, Wx, ba, bx, Lambda, out_0, out_1):
                         emit_w(W_IN_WINDOW)
                         emit(late, LATE_IN_WIN)
             emit(early, len(early))
+            tail_k = 0
             while wq or late:
-                emit_w(2, TAIL_W_ON_V)
-                emit(late, 2)
+                for r in range(TAIL_STEP):
+                    emit_w(1, 0 if tail_k in TAIL_G else TAIL_W_ON_V)
+                    tail_k += 1
+                emit(late, TAIL_STEP, TAIL_RD_LAG)
             while pending:
                 finish_one()
 

@@ -40,12 +40,15 @@ EARLY_PER_SLOT = 0
 EARLY_IN_WINDOW = 8
 LATE_IN_WINDOW = 0
 W_PER_SLOT = 1
-W_IN_WINDOW = 4
+W_IN_WINDOW = 2
 IX_LAG = 1
 SQ_LAG = 1
 SQ_ON_S_FROM = 28
-SQ_S_SLOTS = (3, 7)
+SQ_S_SLOTS = ()
 LAST_SUM = 1
+G_PAIR = 1
+SQ_PAIR = 0
+W_EVERY = 2
 S_SQ_LAG = 1
 HEAD_TBL = 1
 W0_ON_S = 0
@@ -274,6 +277,11 @@ def tile_cell_kernel(tc, xt, ht_minus_1, Wa, Wx, ba, bx, Lambda, out_0, out_1):
                 ta = ta_tiles[s // 4][:, :, s % 4, :]
                 if sq_on_s(s):
                     nc.scalar.activation(out=a2_tiles[s // 4][:, :, s % 4, :], in_=ta, func=ACT.Square)
+                elif SQ_PAIR and s % 4 == 0:
+                    return
+                elif SQ_PAIR and s % 4 == 1:
+                    ta2 = ta_tiles[s // 4][:, :, 0:2, :].rearrange("p j t r -> p j (t r)")
+                    nc.gpsimd.tensor_tensor(out=a2_tiles[s // 4][:, :, 0:2, :].rearrange("p j t r -> p j (t r)"), in0=ta2, in1=ta2, op=ALU.mult)
                 else:
                     nc.gpsimd.tensor_tensor(out=a2_tiles[s // 4][:, :, s % 4, :], in0=ta, in1=ta, op=ALU.mult)
 
@@ -289,16 +297,17 @@ def tile_cell_kernel(tc, xt, ht_minus_1, Wa, Wx, ba, bx, Lambda, out_0, out_1):
                 for k in range(parts):
                     nc.scalar.activation(out=f[:, k * w:(k + 1) * w], in_=f[:, k * w:(k + 1) * w], func=ACT.Sqrt,
                                          scale=-0.25, bias=quarter[:, 0:1])
-                for jj in range(4):
+                for jj in range(0, 4, 1 + G_PAIR):
                     wq.append((n, jj))
 
             def emit_w(k, on_vector=0):
                 for r in range(min(k, len(wq))):
                     n, jj = wq.pop(0)
-                    f = a2_tiles[n][:, jj].rearrange("p c r -> p (c r)")
+                    f = a2_tiles[n][:, jj:jj + 1 + G_PAIR].rearrange("p j c r -> p (j c r)")
                     eng = nc.vector if r < on_vector else nc.gpsimd
-                    eng.tensor_tensor(out=f, in0=f, in1=ix_tiles[n][:, jj].rearrange("p c r -> p (c r)"), op=ALU.mult)
-                    late.append(("s", n, jj))
+                    eng.tensor_tensor(out=f, in0=f, in1=ix_tiles[n][:, jj:jj + 1 + G_PAIR].rearrange("p j c r -> p (j c r)"), op=ALU.mult)
+                    for k2 in range(1 + G_PAIR):
+                        late.append(("s", n, jj + k2))
 
             def do_job(job):
                 kind, n, jj = job
@@ -433,7 +442,8 @@ def tile_cell_kernel(tc, xt, ht_minus_1, Wa, Wx, ba, bx, Lambda, out_0, out_1):
                 emit(late, LATE_PER_SLOT)
                 if fx_now and i == FX_AT + 3 and Q_APART:
                     fx_quant(q + 1)
-                emit_w(W_PER_SLOT)
+                if s % W_EVERY == 0:
+                    emit_w(W_PER_SLOT)
                 if more and MX_MODE == 2:
                     mxp(s + 1, 0)
                 if more and MX_MODE != 1:
@@ -473,7 +483,7 @@ def tile_cell_kernel(tc, xt, ht_minus_1, Wa, Wx, ba, bx, Lambda, out_0, out_1):
                 for r in range(TAIL_STEP):
                     emit_w(1, 0 if tail_k in TAIL_G else TAIL_W_ON_V)
                     tail_k += 1
-                emit(late, TAIL_STEP, TAIL_RD_LAG)
+                emit(late, TAIL_STEP * (1 + G_PAIR), TAIL_RD_LAG)
             while pending:
                 finish_one()
 

@@ -43,7 +43,7 @@ W_PER_SLOT = 1
 W_IN_WINDOW = 2
 IX_LAG = 1
 SQ_LAG = 1
-SQ_ON_S_FROM = 28
+SQ_ON_S_FROM = 32
 SQ_S_SLOTS = ()
 LAST_SUM = 1
 G_PAIR = 1

@@ -64,7 +64,7 @@ W_ON_V = 1
 X_ON_V = 4
 TAIL_W_ON_V = 1
 MX_MODE = 2
-ROOT_PARTS = 1
+ROOT_PARTS = 2
 FX_WINDOW = 0
 LATE_IN_WIN = 0
 

from contextlib import ExitStack

import concourse.mybir as mybir
from concourse.masks import make_identity

FLOPS = 2 * 2048 * 1024 * 2048

F32 = mybir.dt.float32
BF16 = mybir.dt.bfloat16
U32 = mybir.dt.uint32
U8 = mybir.dt.uint8
FP8X4 = mybir.dt.float8_e4m3fn_x4
FP8 = mybir.dt.float8_e4m3fn
ACT = mybir.ActivationFunctionType
ALU = mybir.AluOpType
AX = mybir.AxisListType

P = 128
B = 2048
D = 1024
NJ = B // P
NQ = 4
NC = D // P
NSLOT = NQ * NC
VS = 2752
PIECE = 2048
MX_BUFS = 4
XT_BUFS = 1
TP_BUFS = 3
RUNS = ((0, 1), (2, 3), (4, 5), (6, 7))
A2_BUFS = 3
IX_BUFS = 3
TA_BUFS = 2
TX_BUFS = 3
FX_AT = 2
WL = 3
NWARM = 6
LATE_PER_SLOT = 1
EARLY_PER_SLOT = 0
EARLY_IN_WINDOW = 8
LATE_IN_WINDOW = 0
W_PER_SLOT = 1
W_IN_WINDOW = 2
IX_LAG = 1
SQ_LAG = 1
SQ_ON_S_FROM = 32
SQ_S_SLOTS = ()
LAST_SUM = 1
G_PAIR = 1
SQ_PAIR = 0
W_EVERY = 2
S_SQ_LAG = 1
HEAD_TBL = 1
W0_ON_S = 0
MX0_FIRST = 0
Q_APART = 1
TAIL_RD_LAG = 3
TAIL_G = (0, 2, 4)
TAIL_STEP = 2
RD_LAG = 1
H0_AFTER = 8
X1_AFTER = 12
W_ON_V = 1
X_ON_V = 4
TAIL_W_ON_V = 1
MX_MODE = 2
ROOT_PARTS = 2
FX_WINDOW = 0
LATE_IN_WIN = 0


def tile_cell_kernel(tc, xt, ht_minus_1, Wa, Wx, ba, bx, Lambda, out_0, out_1):
    nc = tc.nc
    x_view = xt.rearrange("(p j) k -> p j k", j=NJ)
    h_view = ht_minus_1.rearrange("(p j) k -> p j k", j=NJ)
    o0_view = out_0.rearrange("(p j) c -> p j c", j=NJ)
    o1_view = out_1.rearrange("(p j) c -> p (j c)", j=NJ)
    w_view = (Wa.rearrange("(b m e) k -> b e m k", b=4, e=2), Wx.rearrange("(b m e) k -> b e m k", b=4, e=2))

    with ExitStack() as ctx:
        ctx.enter_context(tc.manual_schedule())
        const = ctx.enter_context(tc.tile_pool(name="const", bufs=1))
        keep = ctx.enter_context(tc.tile_pool(name="keep", bufs=1))
        share = ctx.enter_context(tc.tile_pool(name="share", bufs=1))
        psum = ctx.enter_context(tc.psum_pool(name="psum", bufs=2))

        w_codes = keep.tile([P, NC, 2, 256], U32, name="w_codes", align_bytes=64)
        w_scales = keep.tile([P, NC, 2, 256], U8, name="w_scales", align_bytes=64)
        stats = const.tile([P, 2 * NJ], F32, name="stats")
        nc.vector.memset(stats[:], 0.0)
        outs = []
        for q in range(2):
            o_q = keep.tile([P, 4, D], F32, name="o_q%d" % q)
            outs.append(o_q)

        wz = const.tile([P, 512], BF16, name="wz")
        nc.vector.memset(wz[:], 0.0)
        for i in range(NWARM):
            wp = psum.tile([P, 512], F32, name="wp", tag="mx", bufs=MX_BUFS)
            nc.tensor.matmul(out=wp[:], lhsT=wz[:, 0:P], rhs=wz[:], start=True, stop=True)
        vecs = const.tile([P, 3, 8, 2], BF16, name="vecs")
        for i, v in enumerate((ba, bx, Lambda)):
            nc.scalar.dma_start(out=vecs[:, i, 0:4, :], in_=v.rearrange("o (b p e) -> p (o b) e", b=4, e=2))
        ident = const.tile([P, P], F32, name="ident")
        make_identity(nc, ident[:])
        zero = const.tile([P, 1], F32, name="zero")
        nc.vector.memset(zero[:], 0.0)
        one = const.tile([P, 1], F32, name="one")
        nc.vector.memset(one[:], 1.0)
        warm = const.tile([P, 1], F32, name="warm")
        if HEAD_TBL:
            nc.scalar.activation(out=warm[:], in_=zero[:], func=ACT.Exp)
        quarter = const.tile([P, 1], F32, name="quarter")
        nc.vector.memset(quarter[:], 0.25)

        with ExitStack() as ph1:
            xraw = ph1.enter_context(tc.tile_pool(name="xraw", bufs=3))
            hraw = ph1.enter_context(tc.tile_pool(name="hraw", bufs=2))
            grp = ph1.enter_context(tc.tile_pool(name="grp", bufs=1))
            xq = ph1.enter_context(tc.tile_pool(name="xq", bufs=2))
            bl = ph1.enter_context(tc.tile_pool(name="bl", bufs=2))

            x_tiles = {}
            h_tiles = {}
            w_tiles = {}
            xg_tiles = {}
            xt_tiles = {}
            xc_tiles = {}
            ta_tiles = {}
            tx_tiles = {}
            a2_tiles = {}
            ix_tiles = {}
            banks = {}
            pending = []
            early = []
            late = []
            wq = []

            def load_x(q):
                xr = xraw.tile([P, 4, D], BF16, name="xr", tag="xr")
                if q == 0:
                    for jj in range(4):
                        nc.sync.dma_start(out=xr[:, jj, :], in_=x_view[:, jj, :])
                else:
                    nc.sync.dma_start(out=xr[:], in_=x_view[:, 4 * q:4 * q + 4, :])
                x_tiles[q] = xr

            def load_h(q):
                hr = hraw.tile([P, 4, D], BF16, name="hr", tag="hr")
                nc.sync.dma_start(out=hr[:], in_=h_view[:, 4 * q:4 * q + 4, :])
                h_tiles[q] = hr

            def load_w(c, gate):
                wr = share.tile([P, D], BF16, name="wr", tag="wr", bufs=2 * NC, offset=0)
                nc.sync.dma_start(out=wr[:], in_=w_view[gate][c // 2, c % 2])
                w_tiles[(c, gate)] = wr

            def turn(rows_bf16):
                words = rows_bf16.bitcast(F32)
                fr = psum.tile([P, 2, 2, P], F32, name="fr", tag="tp", bufs=TP_BUFS)
                for g in range(2):
                    for u in range(2):
                        nc.tensor.transpose(fr[:, g, u, :], words[:, 256 * g + u:256 * (g + 1):2], ident[:])
                return fr[:].rearrange("p g u r -> p g r u")

            def fx_turn(q, jj):
                if jj == 0:
                    xg_tiles[q] = grp.tile([P, 2, 2048], BF16, name="xg", tag="xg", bufs=2, align_bytes=64)
                banks[("fx", q, jj)] = turn(x_tiles[q][:, jj, :])

            def fx_copy(q, jj):
                xgw = xg_tiles[q][:].bitcast(F32)
                dst = xgw[:, :, jj * 256:(jj + 1) * 256].rearrange("p g (r u) -> p g r u", u=2)
                if q == 0 or jj < X_ON_V:
                    nc.vector.tensor_copy(out=dst, in_=banks[("fx", q, jj)])
                else:
                    nc.scalar.copy(out=dst, in_=banks[("fx", q, jj)])

            def xt_turn(s):
                q = s // NC
                c = s % NC
                b = c // 2
                xt = psum.tile([P, 4, P], F32, name="xt", tag="xt", bufs=XT_BUFS)
                for jj in range(4):
                    words = x_tiles[q][:, jj, :].bitcast(F32)
                    nc.tensor.transpose(xt[:, jj, :], words[:, P * b:P * (b + 1)], ident[:])
                xt_tiles[s // 2] = xt
                if c == NC - 2 and q + 3 < NQ:
                    load_x(q + 3)

            def ht_turn(s):
                q = s // NC
                b = (s % NC) // 2
                ht = psum.tile([P, 4, P], F32, name="ht", tag="tp", bufs=TP_BUFS)
                for jj in range(4):
                    words = h_tiles[q][:, jj, :].bitcast(F32)
                    nc.tensor.transpose(ht[:, jj, :], words[:, P * b:P * (b + 1)], ident[:])
                for s2 in (s, s + 1):
                    ta = ta_tiles[s2 // 4][:, :, s2 % 4, :]
                    nc.vector.tensor_tensor(out=ta, in0=ta, in1=ht[:].bitcast(BF16)[:, :, s2 % 2:256:2], op=ALU.mult)

            def fx_quant(q):
                xg = xg_tiles[q]
                xc = xq.tile([P, 2, 512], U32, name="xc", tag="xc", bufs=2, align_bytes=64)
                xs = xq.tile([P, 2, 512], U8, name="xs", tag="xs", bufs=2, align_bytes=64)
                for g in range(2):
                    nc.vector.quantize_mx(out=xc[:, g, :].bitcast(FP8X4), scales=xs[:, g, :], in_=xg[:, g, :])
                xc_tiles[q] = (xc, xs)

            def fw_turn(c):
                for gate in range(2):
                    banks[("fw", c, gate)] = turn(w_tiles[(c, gate)][:])

            def fw_finish(c):
                wg = grp.tile([P, 2, 2, 512], BF16, name="wg", tag="wg", bufs=2, align_bytes=64)
                for gate in range(2):
                    dst = wg[:, gate].bitcast(F32).rearrange("p g (r u) -> p g r u", u=2)
                    if gate < W_ON_V and not (W0_ON_S and c == 0):
                        nc.vector.tensor_copy(out=dst, in_=banks[("fw", c, gate)])
                    else:
                        nc.scalar.copy(out=dst, in_=banks[("fw", c, gate)])
                nc.vector.quantize_mx(
                    out=w_codes[:, c].rearrange("p a n -> p (a n)").bitcast(FP8X4),
                    scales=w_scales[:, c].rearrange("p a n -> p (a n)"),
                    in_=wg[:].rearrange("p a g n -> p (a g n)"),
                )

            def mxp(s, gate):
                q = s // NC
                c = s % NC
                xc, xs = xc_tiles[q]
                acc = psum.tile([P, 512], F32, name="acc", tag="mx", bufs=MX_BUFS)
                for g in range(2):
                    nc.tensor.matmul_mx(
                        out=acc[:],
                        lhsT=w_codes[:, c, gate, g * P:(g + 1) * P].bitcast(FP8X4),
                        lhsT_scale=w_scales[:, c, gate, g * P:(g + 1) * P],
                        rhs=xc[:, g, :].bitcast(FP8X4),
                        rhs_scale=xs[:, g, :],
                        start=(g == 0),
                        stop=(g == 1),
                    )
                banks[("mx", s, gate)] = acc

            def gate_slot(s):
                q = s // NC
                n = s // 4
                t = s % 4
                c = s % NC
                if t == 0:
                    ta_tiles[n] = bl.tile([P, 4, 4, P], F32, name="ta", tag="ta", bufs=TA_BUFS)
                    a2_tiles[n] = bl.tile([P, 4, 4, P], F32, name="a2", tag="a2", bufs=A2_BUFS)
                    ix_tiles[n] = bl.tile([P, 4, 4, P], F32, name="ix", tag="ix", bufs=IX_BUFS)
                ta = ta_tiles[n][:, :, t, :]
                tx = bl.tile([P, 4, P], F32, name="tx", tag="tx", bufs=TX_BUFS)
                tx_tiles[s] = tx
                for gate, dst in ((0, ta), (1, tx[:])):
                    nc.scalar.activation(out=dst, in_=banks[("mx", s, gate)][:].rearrange("p (j r) -> p j r", j=4),
                                         func=ACT.Tanh, scale=0.5, bias=hb[:, gate * NC + c:gate * NC + c + 1])
                    if S_SQ_LAG and gate == 0 and s > 0 and sq_on_s(s - 1) and (s - 1) not in run_at:
                        square(s - 1)
                nc.scalar.activation(out=ta, in_=ta, func=ACT.Exp, scale=nhc[:, c:c + 1], bias=nhc[:, c:c + 1])

            def gated_x(s):
                q = s // NC
                n = s // 4
                t = s % 4
                c = s % NC
                nc.vector.scalar_tensor_tensor(out=ix_tiles[n][:, :, t, :], in0=tx_tiles[s][:], scalar=1.0,
                                               in1=xt_tiles[s // 2][:].bitcast(BF16)[:, :, t % 2:256:2],
                                               op0=ALU.add, op1=ALU.mult)

            def sq_on_s(s):
                return s >= SQ_ON_S_FROM or (s % NC) in SQ_S_SLOTS

            def square(s):
                ta = ta_tiles[s // 4][:, :, s % 4, :]
                if sq_on_s(s):
                    nc.scalar.activation(out=a2_tiles[s // 4][:, :, s % 4, :], in_=ta, func=ACT.Square)
                elif SQ_PAIR and s % 4 == 0:
                    return
                elif SQ_PAIR and s % 4 == 1:
                    ta2 = ta_tiles[s // 4][:, :, 0:2, :].rearrange("p j t r -> p j (t r)")
                    nc.gpsimd.tensor_tensor(out=a2_tiles[s // 4][:, :, 0:2, :].rearrange("p j t r -> p j (t r)"), in0=ta2, in1=ta2, op=ALU.mult)
                else:
                    nc.gpsimd.tensor_tensor(out=a2_tiles[s // 4][:, :, s % 4, :], in0=ta, in1=ta, op=ALU.mult)

            def out_tile(q):
                if q == len(outs):
                    o_late = share.tile([P, 4, D], F32, name="o_late%d" % q, offset=(q - 2) * 16384)
                    outs.append(o_late)
                return outs[q]

            def root(n, parts):
                f = a2_tiles[n][:].rearrange("p j c r -> p (j c r)")
                w = 2048 // parts
                for k in range(parts):
                    nc.scalar.activation(out=f[:, k * w:(k + 1) * w], in_=f[:, k * w:(k + 1) * w], func=ACT.Sqrt,
                                         scale=-0.25, bias=quarter[:, 0:1])
                for jj in range(0, 4, 1 + G_PAIR):
                    wq.append((n, jj))

            def emit_w(k, on_vector=0):
                for r in range(min(k, len(wq))):
                    n, jj = wq.pop(0)
                    f = a2_tiles[n][:, jj:jj + 1 + G_PAIR].rearrange("p j c r -> p (j c r)")
                    eng = nc.vector if r < on_vector else nc.gpsimd
                    eng.tensor_tensor(out=f, in0=f, in1=ix_tiles[n][:, jj:jj + 1 + G_PAIR].rearrange("p j c r -> p (j c r)"), op=ALU.mult)
                    for k2 in range(1 + G_PAIR):
                        late.append(("s", n, jj + k2))

            def do_job(job):
                kind, n, jj = job
                q = n // 2
                half = slice((n % 2) * 512, (n % 2) * 512 + 512)
                bk = psum.tile([P, 4, P], F32, name="bk", tag="tp", bufs=TP_BUFS)
                src = ta_tiles[n] if kind == "a" else a2_tiles[n]
                o = out_tile(q)[:, jj, half].rearrange("p (b m e) -> p b m e", b=2, e=2)
                bkv = bk[:].rearrange("p (b e) m -> p b m e", e=2)
                if LAST_SUM and q == NQ - 1:
                    for t in range(4):
                        nc.tensor.matmul(out=bk[:, t, :], lhsT=ta_tiles[n][:, jj, t, :], rhs=ident[:], is_transpose=True,
                                         start=(t == 0), stop=False)
                    for t in range(4):
                        nc.tensor.matmul(out=bk[:, t, :], lhsT=a2_tiles[n][:, jj, t, :], rhs=ident[:], is_transpose=True,
                                         start=False, stop=(t == 3))
                    nc.scalar.copy(out=o, in_=bkv)
                    pending.append((n, jj))
                    return
                for t in range(4):
                    nc.tensor.transpose(bk[:, t, :], src[:, jj, t, :], ident[:])
                if kind == "a":
                    nc.vector.tensor_tensor(out=o, in0=bkv, in1=h_tiles[q][:, jj, half].rearrange("p (b m e) -> p b m e", b=2, e=2),
                                            op=ALU.mult)
                    if n % 2 == 1 and jj == 3 and q + 2 < NQ:
                        load_h(q + 2)
                else:
                    nc.vector.tensor_tensor(out=o, in0=bkv, in1=o, op=ALU.add)
                    pending.append((n, jj))

            def finish_one():
                n, jj = pending.pop(0)
                q = n // 2
                j = 4 * q + jj
                if q == NQ - 1:
                    half = slice((n % 2) * 512, (n % 2) * 512 + 512)
                    nc.vector.tensor_reduce(out=stats[:, 2 * j + n % 2:2 * j + n % 2 + 1], in_=outs[q][:, jj, half], axis=AX.X,
                                            op=ALU.max, apply_absolute_value=True)
                    if n % 2 == 0:
                        return
                else:
                    if n % 2 == 0:
                        return
                    if jj % 2 == 1:
                        nc.vector.tensor_reduce(out=stats[:, 2 * j:2 * j + 1],
                                                in_=outs[q][:, jj - 1:jj + 1, :].rearrange("p j c -> p (j c)"),
                                                axis=AX.X, op=ALU.max, apply_absolute_value=True)
                nc.sync.dma_start(out=o0_view[:, j, :], in_=outs[q][:, jj, :])

            def emit(queue, k, lag=RD_LAG):
                for r in range(min(k, len(queue))):
                    do_job(queue.pop(0))
                    if len(pending) > lag:
                        finish_one()

            load_x(0)
            for i in range(2 * NC):
                load_w(i // 2, i % 2)
                if i + 1 == H0_AFTER:
                    load_h(0)
                if i + 1 == X1_AFTER:
                    load_x(1)
            load_h(1)
            load_x(2)
            cols24 = const.tile([P, 24], F32, name="cols24")
            nc.vector.tensor_copy(out=cols24[:].rearrange("p (i b e) -> p i b e", i=3, e=2), in_=vecs[:, :, 0:4, :])
            hb = const.tile([P, 16], F32, name="hb")
            nc.vector.tensor_scalar(out=hb[:], in0=cols24[:, 0:16], scalar1=0.5, scalar2=None, op0=ALU.mult)
            lam = cols24[:, 16:24]
            sp_a = const.tile([P, NC], F32, name="sp_a")
            nc.scalar.activation(out=sp_a[:], in_=lam, func=ACT.Abs)
            sp_e = const.tile([P, NC], F32, name="sp_e")
            nc.scalar.activation(out=sp_e[:], in_=sp_a[:], func=ACT.Exp, scale=-1.0)
            sp_l = const.tile([P, NC], F32, name="sp_l")
            nc.scalar.activation(out=sp_l[:], in_=sp_e[:], func=ACT.Ln, bias=one[:, 0:1])
            nc.scalar.activation(out=warm[:], in_=zero[:], func=ACT.Tanh)
            for jj in range(4):
                fx_turn(0, jj)
                fx_copy(0, jj)
            fx_quant(0)
            sp = const.tile([P, NC], F32, name="sp")
            nc.vector.scalar_tensor_tensor(out=sp[:], in0=lam, scalar=0.0, in1=sp_l[:], op0=ALU.max, op1=ALU.add)
            nhc = const.tile([P, NC], F32, name="nhc")
            nc.vector.tensor_scalar(out=nhc[:], in0=sp[:], scalar1=-4.0, scalar2=None, op0=ALU.mult)
            fw_turn(0)
            fw_finish(0)
            if MX0_FIRST:
                mxp(0, 0)
                mxp(0, 1)
            for c in range(1, WL):
                fw_turn(c)
            if not MX0_FIRST:
                mxp(0, 0)
                mxp(0, 1)
            for c in range(1, WL):
                fw_finish(c)

            run_at = {}
            for units in RUNS:
                run_at[4 * units[-1] + 3] = units

            for s in range(NSLOT):
                q = s // NC
                i = s % NC
                more = s + 1 < NSLOT
                if q == 0 and s + WL < NC:
                    fw_turn(s + WL)
                if more and MX_MODE != 2:
                    mxp(s + 1, 0)
                if more and MX_MODE == 1:
                    mxp(s + 1, 1)
                fx_now = q + 1 < NQ and FX_AT <= i < FX_AT + 4 and (q == 0 or not FX_WINDOW)
                if fx_now:
                    fx_turn(q + 1, i - FX_AT)
                if IX_LAG and s > 0:
                    gated_x(s - 1)
                if SQ_LAG and s > 0 and (s - 1) not in run_at and not sq_on_s(s - 1):
                    square(s - 1)
                gate_slot(s)
                if not IX_LAG:
                    gated_x(s)
                if s in run_at and S_SQ_LAG and sq_on_s(s):
                    nc.scalar.activation(out=warm[:], in_=one[:], func=ACT.Sqrt)
                if not SQ_LAG or s in run_at or (sq_on_s(s) and not S_SQ_LAG):
                    square(s)
                if q == 0 and s + WL < NC:
                    fw_finish(s + WL)
                if fx_now:
                    fx_copy(q + 1, i - FX_AT)
                    if i == FX_AT + 3 and not Q_APART:
                        fx_quant(q + 1)
                emit(late, LATE_PER_SLOT)
                if fx_now and i == FX_AT + 3 and Q_APART:
                    fx_quant(q + 1)
                if s % W_EVERY == 0:
                    emit_w(W_PER_SLOT)
                if more and MX_MODE == 2:
                    mxp(s + 1, 0)
                if more and MX_MODE != 1:
                    mxp(s + 1, 1)
                if s % 2 == 0:
                    xt_turn(s)
                emit(early, EARLY_PER_SLOT)
                if LAST_SUM and q == NQ - 1:
                    if i % 2 == 0 and i > 0:
                        ht_turn(s - 2)
                elif s % 4 == 3:
                    for jj in range(4):
                        early.append(("a", s // 4, jj))
                if s in run_at:
                    units = run_at[s]
                    if IX_LAG and not more:
                        gated_x(s)
                    for u in units:
                        root(u, 4 if not more else ROOT_PARTS)
                    if LAST_SUM and not more:
                        ht_turn(s - 1)
                    fx_win = FX_WINDOW and q + 2 < NQ
                    if fx_win:
                        for jj in range(4):
                            fx_turn(q + 2, jj)
                            emit(early, EARLY_IN_WINDOW // 4)
                            fx_copy(q + 2, jj)
                        fx_quant(q + 2)
                    else:
                        emit(early, EARLY_IN_WINDOW)
                    if more:
                        emit_w(W_IN_WINDOW)
                        emit(late, LATE_IN_WIN)
            emit(early, len(early))
            tail_k = 0
            while wq or late:
                for r in range(TAIL_STEP):
                    emit_w(1, 0 if tail_k in TAIL_G else TAIL_W_ON_V)
                    tail_k += 1
                emit(late, TAIL_STEP * (1 + G_PAIR), TAIL_RD_LAG)
            while pending:
                finish_one()

        pm = const.tile([P, 1], F32, name="pm")
        nc.vector.tensor_reduce(out=pm[:], in_=stats[:], axis=AX.X, op=ALU.max)
        tp = psum.tile([P, P], F32, name="tp", tag="tp", bufs=TP_BUFS)
        nc.tensor.transpose(tp[:], pm[:, 0:1].to_broadcast([P, P]), ident[:])
        am = const.tile([P, 1], F32, name="am")
        nc.vector.tensor_reduce(out=am[:], in_=tp[:], axis=AX.X, op=ALU.max)
        rc = const.tile([P, 1], F32, name="rc")
        nc.vector.reciprocal(out=rc[:], in_=am[:])
        fac = const.tile([P, 1], F32, name="fac")
        nc.vector.tensor_scalar(out=fac[:], in0=rc[:], scalar1=448.0, scalar2=None, op0=ALU.mult)

        p2 = ctx.enter_context(tc.tile_pool(name="p2", bufs=4))
        for q in range(NQ):
            flat = outs[q][:].rearrange("p j c -> p (j c)")
            o8 = p2.tile([P, 4096], FP8, name="o8", tag="o8", bufs=4)
            for k in range(4096 // PIECE):
                a = k * PIECE
                m = a + (PIECE * VS) // 4096
                b = a + PIECE
                nc.vector.tensor_scalar(out=o8[:, a:m], in0=flat[:, a:m], scalar1=fac[:, 0:1], scalar2=None,
                                        op0=ALU.mult, saturate=False)
                nc.scalar.activation(out=o8[:, m:b], in_=flat[:, m:b], func=ACT.Identity,
                                     scale=fac[:, 0:1], bias=zero[:, 0:1], saturate=False)
                nc.sync.dma_start(out=o1_view[:, q * 4096 + a:q * 4096 + b], in_=o8[:, a:b].bitcast(U8))
